import numpy as np
import ml_dtypes


def mxq(x, axis, fmt="e4m3"):
    dtype, down = {"e4m3": (ml_dtypes.float8_e4m3fn, 7), "e5m2": (ml_dtypes.float8_e5m2, 14)}[fmt]
    v = np.moveaxis(np.asarray(x, np.float32).astype(ml_dtypes.bfloat16).astype(np.float64), axis, -1)
    blocks = v.reshape(v.shape[:-1] + (-1, 32))
    amax = np.abs(blocks).max(-1, keepdims=True)
    byte = np.maximum(np.where(amax > 0, np.frexp(amax)[1] - 1 + 127, 0) - down, 1)
    scale = np.exp2(byte - 127.0)
    codes = (blocks / scale).astype(np.float32).astype(dtype).astype(np.float64)
    return np.moveaxis((codes * scale).reshape(v.shape), -1, axis)


WIDE = False


def mx_kscale(k):
    if not WIDE:
        return np.ones(k)
    levels = np.array([10, -10, 5, -5, 0])
    a = np.random.permutation(np.resize(levels, k // 512 * 4)).reshape(k // 512, 4)
    idx = np.arange(k)
    return np.exp2(a[idx // 512, idx % 128 // 32])


BF16 = ml_dtypes.bfloat16


def bf(x):
    return np.asarray(x, np.float32).astype(BF16)


def f64(x):
    return np.asarray(x).astype(np.float64)


E2M1 = np.array([0.0, 0.5, 1.0, 1.5, 2.0, 3.0, 4.0, 6.0, -0.0, -0.5, -1.0, -1.5, -2.0, -3.0, -4.0, -6.0])


def pack_weight(w, fmt):
    k, n = w.shape
    w = f64(bf(w)).reshape(k // 32, 32, n)
    amax = np.abs(w).max(1)
    if fmt == "e4m3":
        byte = np.frexp(amax)[1] - 1 + 127 - 7
    else:
        mant, ex = np.frexp(amax / 6.0)
        byte = np.where(mant > 0.5, ex, ex - 1) + 127
    byte = np.clip(np.where(amax > 0, byte, 1), 1, 254)
    scaled = (w * np.exp2(127.0 - byte)[:, None, :]).reshape(k, n).astype(np.float32)
    by_word = np.ascontiguousarray(scaled.reshape(k // 512, 128, 4, n).transpose(0, 1, 3, 2))
    if fmt == "e4m3":
        words = by_word.astype(ml_dtypes.float8_e4m3fn).view(np.uint8)
    else:
        c = by_word.astype(ml_dtypes.float4_e2m1fn).view(np.uint8) & 0xF
        words = c[..., 0::2] | (c[..., 1::2] << 4)
    return np.ascontiguousarray(words), np.ascontiguousarray(byte.astype(np.uint8).reshape(k // 512, 16, n))


def unpack_weight(words, scales, fmt):
    g, p, n, _ = words.shape
    if fmt == "e4m3":
        vals = np.ascontiguousarray(words).view(ml_dtypes.float8_e4m3fn).astype(np.float64)
    else:
        nib = np.empty((g, p, n, 4), np.uint8)
        nib[..., 0::2] = words & 0xF
        nib[..., 1::2] = words >> 4
        vals = E2M1[nib]
    vals = vals * np.repeat(np.exp2(scales.astype(np.float64) - 127.0), 8, axis=1)[..., None]
    return vals.transpose(0, 1, 3, 2).reshape(g * 512, n)


B, P_DIM, H_DIM, X_DIM = 512, 512, 1024, 512
FMT = "e4m3"


def sigmoid(v):
    return 1.0 / (1.0 + np.exp(-v))


def setup_inputs():
    sp, sh, sx = mx_kscale(P_DIM), mx_kscale(H_DIM), mx_kscale(X_DIM)

    def lin_w(in_d, s):
        w = np.random.standard_normal((H_DIM, in_d)) * 0.6 / np.sqrt(in_d) / s[None, :]
        return pack_weight(np.ascontiguousarray(w.T), FMT)

    def lin_b():
        return bf(np.random.standard_normal(H_DIM) * 0.5)

    out = {
        "P": bf(np.random.standard_normal((B, P_DIM)) * sp),
        "hidden": bf(np.random.standard_normal((B, H_DIM)) * sh),
        "cell": bf(np.random.standard_normal((B, H_DIM))),
        "ext_input": bf(np.random.standard_normal((B, X_DIM)) * sx),
    }
    for k in "ifgo":
        out["W_p" + k + "_words"], out["W_p" + k + "_scales"] = lin_w(P_DIM, sp)
        out["b_p" + k] = lin_b()
    for k in "ifgo":
        out["W_h" + k + "_words"], out["W_h" + k + "_scales"] = lin_w(H_DIM, sh)
    for k in "ifgo":
        out["W_x" + k + "_words"], out["W_x" + k + "_scales"] = lin_w(X_DIM, sx)
    return out


def reference(P, hidden, cell, ext_input,
              W_pi_words, W_pi_scales, b_pi, W_pf_words, W_pf_scales, b_pf,
              W_pg_words, W_pg_scales, b_pg, W_po_words, W_po_scales, b_po,
              W_hi_words, W_hi_scales, W_hf_words, W_hf_scales,
              W_hg_words, W_hg_scales, W_ho_words, W_ho_scales,
              W_xi_words, W_xi_scales, W_xf_words, W_xf_scales,
              W_xg_words, W_xg_scales, W_xo_words, W_xo_scales):
    Wp = np.concatenate([unpack_weight(W_pi_words, W_pi_scales, FMT).T, unpack_weight(W_pf_words, W_pf_scales, FMT).T,
                         unpack_weight(W_pg_words, W_pg_scales, FMT).T, unpack_weight(W_po_words, W_po_scales, FMT).T], axis=0)
    bp = np.concatenate([f64(b_pi), f64(b_pf), f64(b_pg), f64(b_po)], axis=0)
    Wh = np.concatenate([unpack_weight(W_hi_words, W_hi_scales, FMT).T, unpack_weight(W_hf_words, W_hf_scales, FMT).T,
                         unpack_weight(W_hg_words, W_hg_scales, FMT).T, unpack_weight(W_ho_words, W_ho_scales, FMT).T], axis=0)
    Wx = np.concatenate([unpack_weight(W_xi_words, W_xi_scales, FMT).T, unpack_weight(W_xf_words, W_xf_scales, FMT).T,
                         unpack_weight(W_xg_words, W_xg_scales, FMT).T, unpack_weight(W_xo_words, W_xo_scales, FMT).T], axis=0)
    gates = ((mxq(f64(P), 1, "e4m3") @ Wp.T) + bp
             + (mxq(f64(hidden), 1, "e4m3") @ Wh.T)
             + (mxq(f64(ext_input), 1, "e4m3") @ Wx.T))
    gi, gf, gg, go = np.split(gates, 4, axis=-1)
    i = sigmoid(gi)
    f = sigmoid(gf)
    g = np.tanh(gg)
    o = sigmoid(go)
    c_new = f * f64(cell) + i * g
    h_new = o * np.tanh(c_new)
    return (h_new, c_new)

@@ -1,0 +1,186 @@
+from contextlib import ExitStack
+
+import concourse.mybir as mybir
+from concourse.masks import make_identity
+
+F32 = mybir.dt.float32
+BF16 = mybir.dt.bfloat16
+I32 = mybir.dt.int32
+U32 = mybir.dt.uint32
+U8 = mybir.dt.uint8
+FP8X4 = mybir.dt.float8_e4m3fn_x4
+ADD = mybir.AluOpType.add
+MULT = mybir.AluOpType.mult
+SIGMOID = mybir.ActivationFunctionType.Sigmoid
+TANH = mybir.ActivationFunctionType.Tanh
+
+PARTS = 128
+BATCH = 512
+HID = 1024
+K_PASS = 512
+K_GROUPS = 4
+M_TILES = BATCH // PARTS
+N_TILE = 512
+HALVES = HID // N_TILE
+QUADS = 4
+
+FLOPS = 2 * BATCH * (K_GROUPS * K_PASS) * (4 * HID)
+
+
+def tile_structuredlstmcell_kernel(
+    tc, P, hidden, cell, ext_input,
+    W_pi_words, W_pi_scales, b_pi, W_pf_words, W_pf_scales, b_pf,
+    W_pg_words, W_pg_scales, b_pg, W_po_words, W_po_scales, b_po,
+    W_hi_words, W_hi_scales, W_hf_words, W_hf_scales,
+    W_hg_words, W_hg_scales, W_ho_words, W_ho_scales,
+    W_xi_words, W_xi_scales, W_xf_words, W_xf_scales,
+    W_xg_words, W_xg_scales, W_xo_words, W_xo_scales,
+    out_0, out_1,
+):
+    nc = tc.nc
+    h_new, c_new = out_0, out_1
+
+    gates = [
+        dict(func=SIGMOID, bias=b_pf, words=(W_pf_words, W_hf_words, W_xf_words),
+             scales=(W_pf_scales, W_hf_scales, W_xf_scales)),
+        dict(func=SIGMOID, bias=b_pi, words=(W_pi_words, W_hi_words, W_xi_words),
+             scales=(W_pi_scales, W_hi_scales, W_xi_scales)),
+        dict(func=TANH, bias=b_pg, words=(W_pg_words, W_hg_words, W_xg_words),
+             scales=(W_pg_scales, W_hg_scales, W_xg_scales)),
+        dict(func=SIGMOID, bias=b_po, words=(W_po_words, W_ho_words, W_xo_words),
+             scales=(W_po_scales, W_ho_scales, W_xo_scales)),
+    ]
+    FORGET, INPUT, CAND, OUTPUT = 0, 1, 2, 3
+    groups = [
+        dict(x=P[:, 0:K_PASS], source=0, part=0),
+        dict(x=hidden[:, 0:K_PASS], source=1, part=0),
+        dict(x=hidden[:, K_PASS:2 * K_PASS], source=1, part=1),
+        dict(x=ext_input[:, 0:K_PASS], source=2, part=0),
+    ]
+
+    with ExitStack() as ctx:
+        keep = ctx.enter_context(tc.tile_pool(name="keep", bufs=1))
+        work = ctx.enter_context(tc.tile_pool(name="work", bufs=4))
+        psum = ctx.enter_context(tc.psum_pool(name="psum", bufs=8))
+
+        x_rows = [keep.tile([PARTS, M_TILES, K_PASS], BF16, name="x_rows%d" % c) for c in range(K_GROUPS)]
+        x_codes = keep.tile([PARTS, K_GROUPS, BATCH], U32, name="x_codes", align_bytes=64)
+        x_scales = keep.tile([PARTS, K_GROUPS, BATCH], U8, name="x_scales", align_bytes=64)
+        w_codes = [[keep.tile([PARTS, HID], U32, name="w_codes%d_%d" % (k, c), align_bytes=64)
+                    for c in range(K_GROUPS)] for k in range(4)]
+        w_scales = [keep.tile([PARTS, K_GROUPS, HID], U8, name="w_scales%d" % k, align_bytes=64)
+                    for k in range(4)]
+        cell_rows = keep.tile([PARTS, M_TILES, HID], BF16, name="cell_rows")
+        bias_rows = keep.tile([PARTS, 4, HID], BF16, name="bias_rows")
+        bias_all = keep.tile([PARTS, 4, HID], BF16, name="bias_all")
+        ones = keep.tile([PARTS, PARTS], BF16, name="ones")
+        ident = keep.tile([PARTS, PARTS], F32, name="ident")
+        forget_all = keep.tile([PARTS, M_TILES, HID], F32, name="forget_all")
+        input_all = keep.tile([PARTS, M_TILES, HID], F32, name="input_all")
+        tanh_c_all = keep.tile([PARTS, M_TILES, HID], F32, name="tanh_c_all")
+
+        nc.vector.memset(w_scales[0][:].bitcast(I32), 0)
+        nc.vector.memset(bias_rows[:], 0.0)
+        nc.vector.memset(ones[:], 1.0)
+        for k in range(1, 4):
+            nc.vector.memset(w_scales[k][:].bitcast(I32), 0)
+        make_identity(nc, ident[:])
+
+        for k in range(4):
+            nc.scalar.dma_start(out=bias_rows[0:1, k, :], in_=gates[k]["bias"].unsqueeze(0))
+
+        for c in range(K_GROUPS):
+            nc.sync.dma_start(out=x_rows[c][:], in_=groups[c]["x"].rearrange("(m p) k -> p m k", p=PARTS))
+
+        def load_scale_rows(k, source):
+            first = [c for c in range(K_GROUPS) if groups[c]["source"] == source][0]
+            count = len([c for c in range(K_GROUPS) if groups[c]["source"] == source])
+            for r in range(4):
+                nc.sync.dma_start(
+                    out=w_scales[k][r:PARTS:32, first:first + count, :].bitcast(I32),
+                    in_=gates[k]["scales"][source][:, r:4 * QUADS:4, :].rearrange("g q n -> q g n").bitcast(I32),
+                )
+
+        def load_codes(k, c):
+            words = gates[k]["words"][groups[c]["source"]][groups[c]["part"]]
+            nc.sync.dma_start(
+                out=w_codes[k][c][:].bitcast(I32),
+                in_=words.rearrange("p n t -> p (n t)").bitcast(I32),
+            )
+
+        for k in range(4):
+            for c in range(K_GROUPS):
+                if groups[c]["part"] == 0:
+                    load_scale_rows(k, groups[c]["source"])
+                load_codes(k, c)
+            if k == FORGET:
+                nc.sync.dma_start(out=cell_rows[:], in_=cell.rearrange("(m p) n -> p m n", p=PARTS))
+
+        for c in range(K_GROUPS):
+            x_words = x_rows[c][:].bitcast(F32)
+            grouped = work.tile([PARTS, 4 * BATCH], BF16, name="grouped", align_bytes=64)
+            grouped_words = grouped[:].bitcast(F32).rearrange("p (b u) -> p b u", u=2)
+            for pair in range(M_TILES // 2):
+                flipped = psum.tile([PARTS, 2, 2 * PARTS], F32, name="flipped", tag="bank")
+                for u in range(2):
+                    for j in range(2):
+                        nc.tensor.transpose(
+                            flipped[:, u, j * PARTS:(j + 1) * PARTS],
+                            x_words[:, 2 * pair + j, u:K_PASS // 2:2],
+                            ident[:],
+                        )
+                rows = slice(pair * 2 * PARTS, (pair + 1) * 2 * PARTS)
+                if pair == 0:
+                    nc.vector.tensor_copy(out=grouped_words[:, rows, :], in_=flipped[:].rearrange("p u b -> p b u"))
+                else:
+                    nc.scalar.copy(out=grouped_words[:, rows, :], in_=flipped[:].rearrange("p u b -> p b u"))
+            nc.vector.quantize_mx(out=x_codes[:, c, :].bitcast(FP8X4), scales=x_scales[:, c, :], in_=grouped[:])
+
+        for k in range(4):
+            spread = psum.tile([PARTS, HID], BF16, name="spread", tag="bank")
+            for half in range(HALVES):
+                cols = slice(half * N_TILE, (half + 1) * N_TILE)
+                nc.tensor.matmul(out=spread[:, cols], lhsT=ones[:], rhs=bias_rows[:, k, cols], start=True, stop=True)
+            nc.scalar.copy(out=bias_all[:, k, :], in_=spread[:])
+
+            for half in range(HALVES):
+                cols = slice(half * N_TILE, (half + 1) * N_TILE)
+                acc = [psum.tile([PARTS, N_TILE], F32, name="acc%d" % m, tag="bank") for m in range(M_TILES)]
+                if k == 0:
+                    order = [(c, m) for c in range(K_GROUPS) for m in range(M_TILES)]
+                else:
+                    order = [(c, m) for m in range(M_TILES) for c in range(K_GROUPS)]
+                for c, m in order:
+                    rows = slice(m * PARTS, (m + 1) * PARTS)
+                    nc.tensor.matmul_mx(
+                        out=acc[m][:],
+                        lhsT=x_codes[:, c, rows].bitcast(FP8X4),
+                        lhsT_scale=x_scales[:, c, rows],
+                        rhs=w_codes[k][c][:, cols].bitcast(FP8X4),
+                        rhs_scale=w_scales[k][:, c, cols],
+                        start=(c == 0),
+                        stop=(c == K_GROUPS - 1),
+                    )
+
+                for m in range(M_TILES):
+                    rows = slice(m * PARTS, (m + 1) * PARTS)
+                    if k == FORGET:
+                        gate = forget_all[:, m, cols]
+                    elif k == INPUT:
+                        gate = input_all[:, m, cols]
+                    else:
+                        gate_tile = work.tile([PARTS, N_TILE], F32, name="gate_tile")
+                        gate = gate_tile[:]
+                    nc.vector.tensor_tensor(out=gate, in0=acc[m][:], in1=bias_all[:, k, cols], op=ADD)
+                    nc.scalar.activation(out=gate, in_=gate, func=gates[k]["func"])
+                    if k == FORGET:
+                        nc.gpsimd.tensor_tensor(out=gate, in0=gate, in1=cell_rows[:, m, cols], op=MULT)
+                    if k == CAND:
+                        nc.gpsimd.tensor_tensor(out=gate, in0=gate, in1=input_all[:, m, cols], op=MULT)
+                        c_tile = work.tile([PARTS, N_TILE], F32, name="c_tile")
+                        nc.vector.tensor_tensor(out=c_tile[:], in0=gate, in1=forget_all[:, m, cols], op=ADD)
+                        nc.sync.dma_start(out=c_new[rows, cols], in_=c_tile[:])
+                        nc.scalar.activation(out=tanh_c_all[:, m, cols], in_=c_tile[:], func=TANH)
+                    if k == OUTPUT:
+                        nc.vector.tensor_tensor(out=gate, in0=gate, in1=tanh_c_all[:, m, cols], op=MULT)
+                        nc.sync.dma_start(out=h_new[rows, cols], in_=gate)

@@ -68,10 +68,9 @@ def tile_structuredlstmcell_kernel(
         x_scales = keep.tile([PARTS, K_GROUPS, BATCH], U8, name="x_scales", align_bytes=64)
         w_codes = [[keep.tile([PARTS, HID], U32, name="w_codes%d_%d" % (k, c), align_bytes=64)
                     for c in range(K_GROUPS)] for k in range(4)]
-        w_scales = [keep.tile([PARTS, K_GROUPS, HID], U8, name="w_scales%d" % k, align_bytes=64)
-                    for k in range(4)]
+        w_scales = keep.tile([PARTS, 4, HID], U8, name="w_scales", align_bytes=64)
         cell_rows = keep.tile([PARTS, M_TILES, HID], BF16, name="cell_rows")
-        bias_rows = keep.tile([PARTS, 4, HID], BF16, name="bias_rows")
+        bias_rows = [keep.tile([PARTS, HID], BF16, name="bias_rows%d" % k) for k in range(4)]
         bias_all = keep.tile([PARTS, 4, HID], BF16, name="bias_all")
         ones = keep.tile([PARTS, PARTS], BF16, name="ones")
         ident = keep.tile([PARTS, PARTS], F32, name="ident")
@@ -79,26 +78,23 @@ def tile_structuredlstmcell_kernel(
         input_all = keep.tile([PARTS, M_TILES, HID], F32, name="input_all")
         tanh_c_all = keep.tile([PARTS, M_TILES, HID], F32, name="tanh_c_all")
 
-        nc.vector.memset(w_scales[0][:].bitcast(I32), 0)
-        nc.vector.memset(bias_rows[:], 0.0)
+        nc.vector.memset(w_scales[:].bitcast(I32), 0)
+        for k in range(4):
+            nc.vector.memset(bias_rows[k][:], 0.0)
         nc.vector.memset(ones[:], 1.0)
-        for k in range(1, 4):
-            nc.vector.memset(w_scales[k][:].bitcast(I32), 0)
         make_identity(nc, ident[:])
 
-        for k in range(4):
-            nc.scalar.dma_start(out=bias_rows[0:1, k, :], in_=gates[k]["bias"].unsqueeze(0))
 
         for c in range(K_GROUPS):
             nc.sync.dma_start(out=x_rows[c][:], in_=groups[c]["x"].rearrange("(m p) k -> p m k", p=PARTS))
 
-        def load_scale_rows(k, source):
+        def load_scale_rows(queue, word, k, source):
             first = [c for c in range(K_GROUPS) if groups[c]["source"] == source][0]
             count = len([c for c in range(K_GROUPS) if groups[c]["source"] == source])
-            for r in range(4):
-                nc.sync.dma_start(
-                    out=w_scales[k][r:PARTS:32, first:first + count, :].bitcast(I32),
-                    in_=gates[k]["scales"][source][:, r:4 * QUADS:4, :].rearrange("g q n -> q g n").bitcast(I32),
+            for quad in range(QUADS):
+                queue.dma_start(
+                    out=w_scales[32 * quad + 4 * first:32 * quad + 4 * (first + count), k, :].bitcast(word),
+                    in_=gates[k]["scales"][source][:, 4 * quad:4 * quad + 4, :].bitcast(word),
                 )
 
         def load_codes(k, c):
@@ -109,9 +105,13 @@ def tile_structuredlstmcell_kernel(
             )
 
         for k in range(4):
+            nc.sync.dma_start(out=bias_rows[k][0:1, :], in_=gates[k]["bias"].unsqueeze(0))
+            for source in range(3):
+                if k < 2 and source != 1:
+                    load_scale_rows(nc.gpsimd, F32, k, source)
+                else:
+                    load_scale_rows(nc.sync, I32, k, source)
             for c in range(K_GROUPS):
-                if groups[c]["part"] == 0:
-                    load_scale_rows(k, groups[c]["source"])
                 load_codes(k, c)
             if k == FORGET:
                 nc.sync.dma_start(out=cell_rows[:], in_=cell.rearrange("(m p) n -> p m n", p=PARTS))
@@ -140,7 +140,7 @@ def tile_structuredlstmcell_kernel(
             spread = psum.tile([PARTS, HID], BF16, name="spread", tag="bank")
             for half in range(HALVES):
                 cols = slice(half * N_TILE, (half + 1) * N_TILE)
-                nc.tensor.matmul(out=spread[:, cols], lhsT=ones[:], rhs=bias_rows[:, k, cols], start=True, stop=True)
+                nc.tensor.matmul(out=spread[:, cols], lhsT=ones[:], rhs=bias_rows[k][:, cols], start=True, stop=True)
             nc.scalar.copy(out=bias_all[:, k, :], in_=spread[:])
 
             for half in range(HALVES):
@@ -157,7 +157,7 @@ def tile_structuredlstmcell_kernel(
                         lhsT=x_codes[:, c, rows].bitcast(FP8X4),
                         lhsT_scale=x_scales[:, c, rows],
                         rhs=w_codes[k][c][:, cols].bitcast(FP8X4),
-                        rhs_scale=w_scales[k][:, c, cols],
+                        rhs_scale=w_scales[4 * c:PARTS, k, cols],
                         start=(c == 0),
                         stop=(c == K_GROUPS - 1),
                     )
@@ -176,7 +176,7 @@ def tile_structuredlstmcell_kernel(
                     if k == FORGET:
                         nc.gpsimd.tensor_tensor(out=gate, in0=gate, in1=cell_rows[:, m, cols], op=MULT)
                     if k == CAND:
-                        nc.gpsimd.tensor_tensor(out=gate, in0=gate, in1=input_all[:, m, cols], op=MULT)
+                        nc.vector.tensor_tensor(out=gate, in0=gate, in1=input_all[:, m, cols], op=MULT)
                         c_tile = work.tile([PARTS, N_TILE], F32, name="c_tile")
                         nc.vector.tensor_tensor(out=c_tile[:], in0=gate, in1=forget_all[:, m, cols], op=ADD)
                         nc.sync.dma_start(out=c_new[rows, cols], in_=c_tile[:])

@@ -23,6 +23,7 @@ M_TILES = BATCH // PARTS
 N_TILE = 512
 HALVES = HID // N_TILE
 QUADS = 4
+LAG = 2
 
 FLOPS = 2 * BATCH * (K_GROUPS * K_PASS) * (4 * HID)
 
@@ -38,7 +39,6 @@ def tile_structuredlstmcell_kernel(
     out_0, out_1,
 ):
     nc = tc.nc
-    h_new, c_new = out_0, out_1
 
     gates = [
         dict(func=SIGMOID, bias=b_pf, words=(W_pf_words, W_hf_words, W_xf_words),
@@ -51,26 +51,29 @@ def tile_structuredlstmcell_kernel(
              scales=(W_po_scales, W_ho_scales, W_xo_scales)),
     ]
     FORGET, INPUT, CAND, OUTPUT = 0, 1, 2, 3
-    groups = [
-        dict(x=P[:, 0:K_PASS], source=0, part=0),
-        dict(x=hidden[:, 0:K_PASS], source=1, part=0),
-        dict(x=hidden[:, K_PASS:2 * K_PASS], source=1, part=1),
-        dict(x=ext_input[:, 0:K_PASS], source=2, part=0),
-    ]
+    sources = [dict(x=P, first=0, count=1), dict(x=hidden, first=1, count=2), dict(x=ext_input, first=3, count=1)]
+
+    def by_partition(ap):
+        return ap.rearrange("(p m) n -> p m n", m=M_TILES)
+
+    h_rows = by_partition(out_0)
+    c_rows = by_partition(out_1)
 
     with ExitStack() as ctx:
+        ctx.enter_context(tc.manual_schedule())
         keep = ctx.enter_context(tc.tile_pool(name="keep", bufs=1))
-        work = ctx.enter_context(tc.tile_pool(name="work", bufs=4))
+        stage = ctx.enter_context(tc.tile_pool(name="stage", bufs=K_GROUPS))
+        work = ctx.enter_context(tc.tile_pool(name="work", bufs=6))
         psum = ctx.enter_context(tc.psum_pool(name="psum", bufs=8))
 
-        x_rows = [keep.tile([PARTS, M_TILES, K_PASS], BF16, name="x_rows%d" % c) for c in range(K_GROUPS)]
+        x_rows = [keep.tile([PARTS, M_TILES, s["count"] * K_PASS], BF16, name="x_rows%d" % s["first"]) for s in sources]
         x_codes = keep.tile([PARTS, K_GROUPS, BATCH], U32, name="x_codes", align_bytes=64)
         x_scales = keep.tile([PARTS, K_GROUPS, BATCH], U8, name="x_scales", align_bytes=64)
         w_codes = [[keep.tile([PARTS, HID], U32, name="w_codes%d_%d" % (k, c), align_bytes=64)
                     for c in range(K_GROUPS)] for k in range(4)]
         w_scales = keep.tile([PARTS, 4, HID], U8, name="w_scales", align_bytes=64)
         cell_rows = keep.tile([PARTS, M_TILES, HID], BF16, name="cell_rows")
-        bias_rows = [keep.tile([PARTS, HID], BF16, name="bias_rows%d" % k) for k in range(4)]
+        bias_rows = keep.tile([PARTS, 4, HID], BF16, name="bias_rows")
         bias_all = keep.tile([PARTS, 4, HID], BF16, name="bias_all")
         ones = keep.tile([PARTS, PARTS], BF16, name="ones")
         ident = keep.tile([PARTS, PARTS], F32, name="ident")
@@ -79,54 +82,60 @@ def tile_structuredlstmcell_kernel(
         tanh_c_all = keep.tile([PARTS, M_TILES, HID], F32, name="tanh_c_all")
 
         nc.vector.memset(w_scales[:].bitcast(I32), 0)
-        for k in range(4):
-            nc.vector.memset(bias_rows[k][:], 0.0)
+        nc.vector.memset(bias_rows[:], 0.0)
         nc.vector.memset(ones[:], 1.0)
         make_identity(nc, ident[:])
 
+        def load_x(s):
+            nc.sync.dma_start(out=x_rows[s][:], in_=by_partition(sources[s]["x"]))
 
-        for c in range(K_GROUPS):
-            nc.sync.dma_start(out=x_rows[c][:], in_=groups[c]["x"].rearrange("(m p) k -> p m k", p=PARTS))
-
-        def load_scale_rows(queue, word, k, source):
-            first = [c for c in range(K_GROUPS) if groups[c]["source"] == source][0]
-            count = len([c for c in range(K_GROUPS) if groups[c]["source"] == source])
+        def load_scale_rows(k, s):
+            first, count = sources[s]["first"], sources[s]["count"]
             for quad in range(QUADS):
-                queue.dma_start(
-                    out=w_scales[32 * quad + 4 * first:32 * quad + 4 * (first + count), k, :].bitcast(word),
-                    in_=gates[k]["scales"][source][:, 4 * quad:4 * quad + 4, :].bitcast(word),
+                nc.sync.dma_start(
+                    out=w_scales[32 * quad + 4 * first:32 * quad + 4 * (first + count), k, :].bitcast(I32),
+                    in_=gates[k]["scales"][s][:, 4 * quad:4 * quad + 4, :].bitcast(I32),
                 )
 
-        def load_codes(k, c):
-            words = gates[k]["words"][groups[c]["source"]][groups[c]["part"]]
-            nc.sync.dma_start(
-                out=w_codes[k][c][:].bitcast(I32),
-                in_=words.rearrange("p n t -> p (n t)").bitcast(I32),
-            )
+        def load_codes(k, s):
+            for part in range(sources[s]["count"]):
+                nc.sync.dma_start(
+                    out=w_codes[k][sources[s]["first"] + part][:].bitcast(I32),
+                    in_=gates[k]["words"][s][part].rearrange("p n t -> p (n t)").bitcast(I32),
+                )
 
         for k in range(4):
-            nc.sync.dma_start(out=bias_rows[k][0:1, :], in_=gates[k]["bias"].unsqueeze(0))
-            for source in range(3):
-                if k < 2 and source != 1:
-                    load_scale_rows(nc.gpsimd, F32, k, source)
-                else:
-                    load_scale_rows(nc.sync, I32, k, source)
-            for c in range(K_GROUPS):
-                load_codes(k, c)
-            if k == FORGET:
-                nc.sync.dma_start(out=cell_rows[:], in_=cell.rearrange("(m p) n -> p m n", p=PARTS))
+            nc.gpsimd.dma_start(out=bias_rows[0:1, k, :], in_=gates[k]["bias"].unsqueeze(0))
+
+        load_x(0)
+        load_x(1)
+        load_scale_rows(FORGET, 0)
+        load_x(2)
+        for k in range(4):
+            for s in range(3):
+                if (k, s) != (FORGET, 0):
+                    load_scale_rows(k, s)
+                load_codes(k, s)
+            if k == INPUT:
+                nc.sync.dma_start(out=cell_rows[:], in_=by_partition(cell))
+
+        grouped = [stage.tile([PARTS, 4 * BATCH], BF16, name="grouped", align_bytes=64) for c in range(K_GROUPS)]
+
+        def quantise(c):
+            nc.vector.quantize_mx(out=x_codes[:, c, :].bitcast(FP8X4), scales=x_scales[:, c, :], in_=grouped[c][:])
 
         for c in range(K_GROUPS):
-            x_words = x_rows[c][:].bitcast(F32)
-            grouped = work.tile([PARTS, 4 * BATCH], BF16, name="grouped", align_bytes=64)
-            grouped_words = grouped[:].bitcast(F32).rearrange("p (b u) -> p b u", u=2)
+            s = [j for j in range(3) if sources[j]["first"] <= c < sources[j]["first"] + sources[j]["count"]][0]
+            word0 = (c - sources[s]["first"]) * K_PASS // 2
+            x_words = x_rows[s][:].bitcast(F32)
+            grouped_words = grouped[c][:].bitcast(F32).rearrange("p (b u) -> p b u", u=2)
             for pair in range(M_TILES // 2):
                 flipped = psum.tile([PARTS, 2, 2 * PARTS], F32, name="flipped", tag="bank")
                 for u in range(2):
                     for j in range(2):
                         nc.tensor.transpose(
                             flipped[:, u, j * PARTS:(j + 1) * PARTS],
-                            x_words[:, 2 * pair + j, u:K_PASS // 2:2],
+                            x_words[:, 2 * pair + j, word0 + u:word0 + K_PASS // 2:2],
                             ident[:],
                         )
                 rows = slice(pair * 2 * PARTS, (pair + 1) * 2 * PARTS)
@@ -134,19 +143,52 @@ def tile_structuredlstmcell_kernel(
                     nc.vector.tensor_copy(out=grouped_words[:, rows, :], in_=flipped[:].rearrange("p u b -> p b u"))
                 else:
                     nc.scalar.copy(out=grouped_words[:, rows, :], in_=flipped[:].rearrange("p u b -> p b u"))
-            nc.vector.quantize_mx(out=x_codes[:, c, :].bitcast(FP8X4), scales=x_scales[:, c, :], in_=grouped[:])
+            if c > 0:
+                quantise(c - 1)
+        quantise(K_GROUPS - 1)
 
-        for k in range(4):
+        def spread_bias(k):
             spread = psum.tile([PARTS, HID], BF16, name="spread", tag="bank")
             for half in range(HALVES):
                 cols = slice(half * N_TILE, (half + 1) * N_TILE)
-                nc.tensor.matmul(out=spread[:, cols], lhsT=ones[:], rhs=bias_rows[k][:, cols], start=True, stop=True)
+                nc.tensor.matmul(out=spread[:, cols], lhsT=ones[:], rhs=bias_rows[:, k, cols], start=True, stop=True)
             nc.scalar.copy(out=bias_all[:, k, :], in_=spread[:])
 
+        def start_bank(k, half, m, acc):
+            cols = slice(half * N_TILE, (half + 1) * N_TILE)
+            if k == FORGET:
+                gate = forget_all[:, m, cols]
+            elif k == INPUT:
+                gate = input_all[:, m, cols]
+            else:
+                gate_tile = work.tile([PARTS, N_TILE], F32, name="gate_tile")
+                gate = gate_tile[:]
+            nc.vector.tensor_tensor(out=gate, in0=acc[:], in1=bias_all[:, k, cols], op=ADD)
+            nc.scalar.activation(out=gate, in_=gate, func=gates[k]["func"])
+            if k == FORGET:
+                nc.gpsimd.tensor_tensor(out=gate, in0=gate, in1=cell_rows[:, m, cols], op=MULT)
+            if k == CAND:
+                nc.gpsimd.tensor_tensor(out=gate, in0=gate, in1=input_all[:, m, cols], op=MULT)
+            return dict(k=k, m=m, cols=cols, gate=gate)
+
+        def end_bank(bank):
+            m, cols, gate = bank["m"], bank["cols"], bank["gate"]
+            if bank["k"] == CAND:
+                c_tile = work.tile([PARTS, N_TILE], F32, name="c_tile")
+                nc.vector.tensor_tensor(out=c_tile[:], in0=gate, in1=forget_all[:, m, cols], op=ADD)
+                nc.sync.dma_start(out=c_rows[:, m, cols], in_=c_tile[:])
+                nc.scalar.activation(out=tanh_c_all[:, m, cols], in_=c_tile[:], func=TANH)
+            if bank["k"] == OUTPUT:
+                nc.vector.tensor_tensor(out=gate, in0=gate, in1=tanh_c_all[:, m, cols], op=MULT)
+                nc.sync.dma_start(out=h_rows[:, m, cols], in_=gate)
+
+        banks = []
+        spread_bias(0)
+        for k in range(4):
             for half in range(HALVES):
                 cols = slice(half * N_TILE, (half + 1) * N_TILE)
                 acc = [psum.tile([PARTS, N_TILE], F32, name="acc%d" % m, tag="bank") for m in range(M_TILES)]
-                if k == 0:
+                if (k, half) == (0, 0):
                     order = [(c, m) for c in range(K_GROUPS) for m in range(M_TILES)]
                 else:
                     order = [(c, m) for m in range(M_TILES) for c in range(K_GROUPS)]
@@ -161,26 +203,11 @@ def tile_structuredlstmcell_kernel(
                         start=(c == 0),
                         stop=(c == K_GROUPS - 1),
                     )
-
                 for m in range(M_TILES):
-                    rows = slice(m * PARTS, (m + 1) * PARTS)
-                    if k == FORGET:
-                        gate = forget_all[:, m, cols]
-                    elif k == INPUT:
-                        gate = input_all[:, m, cols]
-                    else:
-                        gate_tile = work.tile([PARTS, N_TILE], F32, name="gate_tile")
-                        gate = gate_tile[:]
-                    nc.vector.tensor_tensor(out=gate, in0=acc[m][:], in1=bias_all[:, k, cols], op=ADD)
-                    nc.scalar.activation(out=gate, in_=gate, func=gates[k]["func"])
-                    if k == FORGET:
-                        nc.gpsimd.tensor_tensor(out=gate, in0=gate, in1=cell_rows[:, m, cols], op=MULT)
-                    if k == CAND:
-                        nc.vector.tensor_tensor(out=gate, in0=gate, in1=input_all[:, m, cols], op=MULT)
-                        c_tile = work.tile([PARTS, N_TILE], F32, name="c_tile")
-                        nc.vector.tensor_tensor(out=c_tile[:], in0=gate, in1=forget_all[:, m, cols], op=ADD)
-                        nc.sync.dma_start(out=c_new[rows, cols], in_=c_tile[:])
-                        nc.scalar.activation(out=tanh_c_all[:, m, cols], in_=c_tile[:], func=TANH)
-                    if k == OUTPUT:
-                        nc.vector.tensor_tensor(out=gate, in0=gate, in1=tanh_c_all[:, m, cols], op=MULT)
-                        nc.sync.dma_start(out=h_new[rows, cols], in_=gate)
+                    banks.append(start_bank(k, half, m, acc[m]))
+                    if len(banks) > LAG:
+                        end_bank(banks[len(banks) - 1 - LAG])
+                if half == 0 and k + 1 < 4:
+                    spread_bias(k + 1)
+        for bank in banks[len(banks) - LAG:]:
+            end_bank(bank)

@@ -116,8 +116,15 @@ def tile_structuredlstmcell_kernel(
                 if (k, s) != (FORGET, 0):
                     load_scale_rows(k, s)
                 load_codes(k, s)
-            if k == INPUT:
+            if k == FORGET:
                 nc.sync.dma_start(out=cell_rows[:], in_=by_partition(cell))
+
+        def spread_bias(k):
+            spread = psum.tile([PARTS, HID], BF16, name="spread", tag="bank")
+            for half in range(HALVES):
+                cols = slice(half * N_TILE, (half + 1) * N_TILE)
+                nc.tensor.matmul(out=spread[:, cols], lhsT=ones[:], rhs=bias_rows[:, k, cols], start=True, stop=True)
+            nc.scalar.copy(out=bias_all[:, k, :], in_=spread[:])
 
         grouped = [stage.tile([PARTS, 4 * BATCH], BF16, name="grouped", align_bytes=64) for c in range(K_GROUPS)]
 
@@ -143,16 +150,11 @@ def tile_structuredlstmcell_kernel(
                     nc.vector.tensor_copy(out=grouped_words[:, rows, :], in_=flipped[:].rearrange("p u b -> p b u"))
                 else:
                     nc.scalar.copy(out=grouped_words[:, rows, :], in_=flipped[:].rearrange("p u b -> p b u"))
-            if c > 0:
+            if c == 0:
+                spread_bias(0)
+            else:
                 quantise(c - 1)
         quantise(K_GROUPS - 1)
-
-        def spread_bias(k):
-            spread = psum.tile([PARTS, HID], BF16, name="spread", tag="bank")
-            for half in range(HALVES):
-                cols = slice(half * N_TILE, (half + 1) * N_TILE)
-                nc.tensor.matmul(out=spread[:, cols], lhsT=ones[:], rhs=bias_rows[:, k, cols], start=True, stop=True)
-            nc.scalar.copy(out=bias_all[:, k, :], in_=spread[:])
 
         def start_bank(k, half, m, acc):
             cols = slice(half * N_TILE, (half + 1) * N_TILE)
@@ -167,28 +169,32 @@ def tile_structuredlstmcell_kernel(
             nc.scalar.activation(out=gate, in_=gate, func=gates[k]["func"])
             if k == FORGET:
                 nc.gpsimd.tensor_tensor(out=gate, in0=gate, in1=cell_rows[:, m, cols], op=MULT)
-            if k == CAND:
+            if k == CAND and m % 2 == 0:
                 nc.gpsimd.tensor_tensor(out=gate, in0=gate, in1=input_all[:, m, cols], op=MULT)
+            if k == OUTPUT and m % 2 == 0:
+                nc.gpsimd.tensor_tensor(out=gate, in0=gate, in1=tanh_c_all[:, m, cols], op=MULT)
             return dict(k=k, m=m, cols=cols, gate=gate)
 
         def end_bank(bank):
             m, cols, gate = bank["m"], bank["cols"], bank["gate"]
             if bank["k"] == CAND:
+                if m % 2 == 1:
+                    nc.vector.tensor_tensor(out=gate, in0=gate, in1=input_all[:, m, cols], op=MULT)
                 c_tile = work.tile([PARTS, N_TILE], F32, name="c_tile")
                 nc.vector.tensor_tensor(out=c_tile[:], in0=gate, in1=forget_all[:, m, cols], op=ADD)
                 nc.sync.dma_start(out=c_rows[:, m, cols], in_=c_tile[:])
                 nc.scalar.activation(out=tanh_c_all[:, m, cols], in_=c_tile[:], func=TANH)
             if bank["k"] == OUTPUT:
-                nc.vector.tensor_tensor(out=gate, in0=gate, in1=tanh_c_all[:, m, cols], op=MULT)
+                if m % 2 == 1:
+                    nc.vector.tensor_tensor(out=gate, in0=gate, in1=tanh_c_all[:, m, cols], op=MULT)
                 nc.sync.dma_start(out=h_rows[:, m, cols], in_=gate)
 
         banks = []
-        spread_bias(0)
         for k in range(4):
             for half in range(HALVES):
                 cols = slice(half * N_TILE, (half + 1) * N_TILE)
                 acc = [psum.tile([PARTS, N_TILE], F32, name="acc%d" % m, tag="bank") for m in range(M_TILES)]
-                if (k, half) == (0, 0):
+                if k < 2 and half == 0:
                     order = [(c, m) for c in range(K_GROUPS) for m in range(M_TILES)]
                 else:
                     order = [(c, m) for m in range(M_TILES) for c in range(K_GROUPS)]

@@ -109,12 +109,14 @@ def tile_structuredlstmcell_kernel(
 
         load_x(0)
         load_x(1)
-        load_scale_rows(FORGET, 0)
+        for s in range(3):
+            load_scale_rows(FORGET, s)
         load_x(2)
         for k in range(4):
             for s in range(3):
-                if (k, s) != (FORGET, 0):
+                if k != FORGET:
                     load_scale_rows(k, s)
+            for s in range(3):
                 load_codes(k, s)
             if k == FORGET:
                 nc.sync.dma_start(out=cell_rows[:], in_=by_partition(cell))

@@ -52,6 +52,7 @@ def tile_structuredlstmcell_kernel(
     ]
     FORGET, INPUT, CAND, OUTPUT = 0, 1, 2, 3
     sources = [dict(x=P, first=0, count=1), dict(x=hidden, first=1, count=2), dict(x=ext_input, first=3, count=1)]
+    source_of = [0, 1, 1, 2]
 
     def by_partition(ap):
         return ap.rearrange("(p m) n -> p m n", m=M_TILES)
@@ -69,9 +70,9 @@ def tile_structuredlstmcell_kernel(
         x_rows = [keep.tile([PARTS, M_TILES, s["count"] * K_PASS], BF16, name="x_rows%d" % s["first"]) for s in sources]
         x_codes = keep.tile([PARTS, K_GROUPS, BATCH], U32, name="x_codes", align_bytes=64)
         x_scales = keep.tile([PARTS, K_GROUPS, BATCH], U8, name="x_scales", align_bytes=64)
-        w_codes = [[keep.tile([PARTS, HID], U32, name="w_codes%d_%d" % (k, c), align_bytes=64)
-                    for c in range(K_GROUPS)] for k in range(4)]
-        w_scales = keep.tile([PARTS, 4, HID], U8, name="w_scales", align_bytes=64)
+        w_codes = [[keep.tile([PARTS, s["count"], HID], U32, name="w_codes%d_%d" % (k, s["first"]), align_bytes=64)
+                    for s in sources] for k in range(4)]
+        w_scales = [keep.tile([PARTS, 4, HID], U8, name="w_scales%d" % s["first"], align_bytes=64) for s in sources]
         cell_rows = keep.tile([PARTS, M_TILES, HID], BF16, name="cell_rows")
         bias_rows = keep.tile([PARTS, 4, HID], BF16, name="bias_rows")
         bias_all = keep.tile([PARTS, 4, HID], BF16, name="bias_all")
@@ -81,8 +82,9 @@ def tile_structuredlstmcell_kernel(
         input_all = keep.tile([PARTS, M_TILES, HID], F32, name="input_all")
         tanh_c_all = keep.tile([PARTS, M_TILES, HID], F32, name="tanh_c_all")
 
-        nc.vector.memset(w_scales[:].bitcast(I32), 0)
         nc.vector.memset(bias_rows[:], 0.0)
+        for s in range(3):
+            nc.vector.memset(w_scales[s][:].bitcast(I32), 0)
         nc.vector.memset(ones[:], 1.0)
         make_identity(nc, ident[:])
 
@@ -93,31 +95,25 @@ def tile_structuredlstmcell_kernel(
             first, count = sources[s]["first"], sources[s]["count"]
             for quad in range(QUADS):
                 nc.sync.dma_start(
-                    out=w_scales[32 * quad + 4 * first:32 * quad + 4 * (first + count), k, :].bitcast(I32),
+                    out=w_scales[s][32 * quad + 4 * first:32 * quad + 4 * (first + count), k, :].bitcast(I32),
                     in_=gates[k]["scales"][s][:, 4 * quad:4 * quad + 4, :].bitcast(I32),
                 )
 
         def load_codes(k, s):
-            for part in range(sources[s]["count"]):
-                nc.sync.dma_start(
-                    out=w_codes[k][sources[s]["first"] + part][:].bitcast(I32),
-                    in_=gates[k]["words"][s][part].rearrange("p n t -> p (n t)").bitcast(I32),
-                )
+            nc.sync.dma_start(
+                out=w_codes[k][s][:].bitcast(I32),
+                in_=gates[k]["words"][s].rearrange("g p n t -> p g (n t)").bitcast(I32),
+            )
 
         for k in range(4):
             nc.gpsimd.dma_start(out=bias_rows[0:1, k, :], in_=gates[k]["bias"].unsqueeze(0))
 
-        load_x(0)
-        load_x(1)
         for s in range(3):
-            load_scale_rows(FORGET, s)
-        load_x(2)
+            load_x(s)
         for k in range(4):
             for s in range(3):
-                if k != FORGET:
-                    load_scale_rows(k, s)
-            for s in range(3):
                 load_codes(k, s)
+                load_scale_rows(k, s)
             if k == FORGET:
                 nc.sync.dma_start(out=cell_rows[:], in_=by_partition(cell))
 
@@ -134,7 +130,7 @@ def tile_structuredlstmcell_kernel(
             nc.vector.quantize_mx(out=x_codes[:, c, :].bitcast(FP8X4), scales=x_scales[:, c, :], in_=grouped[c][:])
 
         for c in range(K_GROUPS):
-            s = [j for j in range(3) if sources[j]["first"] <= c < sources[j]["first"] + sources[j]["count"]][0]
+            s = source_of[c]
             word0 = (c - sources[s]["first"]) * K_PASS // 2
             x_words = x_rows[s][:].bitcast(F32)
             grouped_words = grouped[c][:].bitcast(F32).rearrange("p (b u) -> p b u", u=2)
@@ -152,11 +148,10 @@ def tile_structuredlstmcell_kernel(
                     nc.vector.tensor_copy(out=grouped_words[:, rows, :], in_=flipped[:].rearrange("p u b -> p b u"))
                 else:
                     nc.scalar.copy(out=grouped_words[:, rows, :], in_=flipped[:].rearrange("p u b -> p b u"))
-            if c == 0:
-                spread_bias(0)
-            else:
+            if c > 0:
                 quantise(c - 1)
         quantise(K_GROUPS - 1)
+        spread_bias(0)
 
         def start_bank(k, half, m, acc):
             cols = slice(half * N_TILE, (half + 1) * N_TILE)
@@ -202,12 +197,13 @@ def tile_structuredlstmcell_kernel(
                     order = [(c, m) for m in range(M_TILES) for c in range(K_GROUPS)]
                 for c, m in order:
                     rows = slice(m * PARTS, (m + 1) * PARTS)
+                    s = source_of[c]
                     nc.tensor.matmul_mx(
                         out=acc[m][:],
                         lhsT=x_codes[:, c, rows].bitcast(FP8X4),
                         lhsT_scale=x_scales[:, c, rows],
-                        rhs=w_codes[k][c][:, cols].bitcast(FP8X4),
-                        rhs_scale=w_scales[4 * c:PARTS, k, cols],
+                        rhs=w_codes[k][s][:, c - sources[s]["first"], cols].bitcast(FP8X4),
+                        rhs_scale=w_scales[s][4 * c:PARTS, k, cols],
                         start=(c == 0),
                         stop=(c == K_GROUPS - 1),
                     )

@@ -23,7 +23,7 @@ M_TILES = BATCH // PARTS
 N_TILE = 512
 HALVES = HID // N_TILE
 QUADS = 4
-LAG = 2
+UNITS = HALVES * M_TILES
 
 FLOPS = 2 * BATCH * (K_GROUPS * K_PASS) * (4 * HID)
 
@@ -64,7 +64,6 @@ def tile_structuredlstmcell_kernel(
         ctx.enter_context(tc.manual_schedule())
         keep = ctx.enter_context(tc.tile_pool(name="keep", bufs=1))
         stage = ctx.enter_context(tc.tile_pool(name="stage", bufs=K_GROUPS))
-        work = ctx.enter_context(tc.tile_pool(name="work", bufs=6))
         psum = ctx.enter_context(tc.psum_pool(name="psum", bufs=8))
 
         x_rows = [keep.tile([PARTS, M_TILES, s["count"] * K_PASS], BF16, name="x_rows%d" % s["first"]) for s in sources]
@@ -78,9 +77,7 @@ def tile_structuredlstmcell_kernel(
         bias_all = keep.tile([PARTS, 4, HID], BF16, name="bias_all")
         ones = keep.tile([PARTS, PARTS], BF16, name="ones")
         ident = keep.tile([PARTS, PARTS], F32, name="ident")
-        forget_all = keep.tile([PARTS, M_TILES, HID], F32, name="forget_all")
-        input_all = keep.tile([PARTS, M_TILES, HID], F32, name="input_all")
-        tanh_c_all = keep.tile([PARTS, M_TILES, HID], F32, name="tanh_c_all")
+        value = [keep.tile([PARTS, M_TILES, HID], F32, name="value%d" % k) for k in range(4)]
 
         nc.vector.memset(bias_rows[:], 0.0)
         for s in range(3):
@@ -153,65 +150,71 @@ def tile_structuredlstmcell_kernel(
         quantise(K_GROUPS - 1)
         spread_bias(0)
 
-        def start_bank(k, half, m, acc):
-            cols = slice(half * N_TILE, (half + 1) * N_TILE)
-            if k == FORGET:
-                gate = forget_all[:, m, cols]
-            elif k == INPUT:
-                gate = input_all[:, m, cols]
+        def cols_of(u):
+            return slice((u // M_TILES) * N_TILE, (u // M_TILES + 1) * N_TILE)
+
+        def at(k, u):
+            return value[k][:, u % M_TILES, cols_of(u)]
+
+        def passes(k, u, acc, groups):
+            rows = slice((u % M_TILES) * PARTS, (u % M_TILES + 1) * PARTS)
+            for c in groups:
+                s = source_of[c]
+                nc.tensor.matmul_mx(
+                    out=acc[:],
+                    lhsT=x_codes[:, c, rows].bitcast(FP8X4),
+                    lhsT_scale=x_scales[:, c, rows],
+                    rhs=w_codes[k][s][:, c - sources[s]["first"], cols_of(u)].bitcast(FP8X4),
+                    rhs_scale=w_scales[s][4 * c:PARTS, k, cols_of(u)],
+                    start=(c == 0),
+                    stop=(c == K_GROUPS - 1),
+                )
+
+        def empty_bank(k, u, acc):
+            nc.vector.tensor_tensor(out=at(k, u), in0=acc[:], in1=bias_all[:, k, cols_of(u)], op=ADD)
+            nc.scalar.activation(out=at(k, u), in_=at(k, u), func=gates[k]["func"])
+
+        for k, half, next_bias in ((FORGET, 0, INPUT), (FORGET, 1, CAND), (INPUT, 0, OUTPUT)):
+            units = [half * M_TILES + m for m in range(M_TILES)]
+            accs = [psum.tile([PARTS, N_TILE], F32, name="acc%d" % m, tag="bank") for m in range(M_TILES)]
+            if half == 0:
+                for c in range(K_GROUPS):
+                    for m, u in enumerate(units):
+                        passes(k, u, accs[m], [c])
             else:
-                gate_tile = work.tile([PARTS, N_TILE], F32, name="gate_tile")
-                gate = gate_tile[:]
-            nc.vector.tensor_tensor(out=gate, in0=acc[:], in1=bias_all[:, k, cols], op=ADD)
-            nc.scalar.activation(out=gate, in_=gate, func=gates[k]["func"])
-            if k == FORGET:
-                nc.gpsimd.tensor_tensor(out=gate, in0=gate, in1=cell_rows[:, m, cols], op=MULT)
-            if k == CAND and m % 2 == 0:
-                nc.gpsimd.tensor_tensor(out=gate, in0=gate, in1=input_all[:, m, cols], op=MULT)
-            if k == OUTPUT and m % 2 == 0:
-                nc.gpsimd.tensor_tensor(out=gate, in0=gate, in1=tanh_c_all[:, m, cols], op=MULT)
-            return dict(k=k, m=m, cols=cols, gate=gate)
+                for m, u in enumerate(units):
+                    passes(k, u, accs[m], range(K_GROUPS))
+            for m, u in enumerate(units):
+                empty_bank(k, u, accs[m])
+                if k == FORGET:
+                    nc.gpsimd.tensor_tensor(out=at(FORGET, u), in0=at(FORGET, u), in1=cell_rows[:, u % M_TILES, cols_of(u)], op=MULT)
+            spread_bias(next_bias)
 
-        def end_bank(bank):
-            m, cols, gate = bank["m"], bank["cols"], bank["gate"]
-            if bank["k"] == CAND:
-                if m % 2 == 1:
-                    nc.vector.tensor_tensor(out=gate, in0=gate, in1=input_all[:, m, cols], op=MULT)
-                c_tile = work.tile([PARTS, N_TILE], F32, name="c_tile")
-                nc.vector.tensor_tensor(out=c_tile[:], in0=gate, in1=forget_all[:, m, cols], op=ADD)
-                nc.sync.dma_start(out=c_rows[:, m, cols], in_=c_tile[:])
-                nc.scalar.activation(out=tanh_c_all[:, m, cols], in_=c_tile[:], func=TANH)
-            if bank["k"] == OUTPUT:
-                if m % 2 == 1:
-                    nc.vector.tensor_tensor(out=gate, in0=gate, in1=tanh_c_all[:, m, cols], op=MULT)
-                nc.sync.dma_start(out=h_rows[:, m, cols], in_=gate)
-
-        banks = []
-        for k in range(4):
-            for half in range(HALVES):
-                cols = slice(half * N_TILE, (half + 1) * N_TILE)
-                acc = [psum.tile([PARTS, N_TILE], F32, name="acc%d" % m, tag="bank") for m in range(M_TILES)]
-                if k < 2 and half == 0:
-                    order = [(c, m) for c in range(K_GROUPS) for m in range(M_TILES)]
-                else:
-                    order = [(c, m) for m in range(M_TILES) for c in range(K_GROUPS)]
-                for c, m in order:
-                    rows = slice(m * PARTS, (m + 1) * PARTS)
-                    s = source_of[c]
-                    nc.tensor.matmul_mx(
-                        out=acc[m][:],
-                        lhsT=x_codes[:, c, rows].bitcast(FP8X4),
-                        lhsT_scale=x_scales[:, c, rows],
-                        rhs=w_codes[k][s][:, c - sources[s]["first"], cols].bitcast(FP8X4),
-                        rhs_scale=w_scales[s][4 * c:PARTS, k, cols],
-                        start=(c == 0),
-                        stop=(c == K_GROUPS - 1),
-                    )
-                for m in range(M_TILES):
-                    banks.append(start_bank(k, half, m, acc[m]))
-                    if len(banks) > LAG:
-                        end_bank(banks[len(banks) - 1 - LAG])
-                if half == 0 and k + 1 < 4:
-                    spread_bias(k + 1)
-        for bank in banks[len(banks) - LAG:]:
-            end_bank(bank)
+        steps = [[(INPUT,4),(INPUT,5)],[(CAND,0),(CAND,1)],[(INPUT,6),(CAND,2)],[(INPUT,7),(CAND,3)],[(CAND,4),(OUTPUT,0)],[(CAND,5),(OUTPUT,1)],[(CAND,6),(OUTPUT,2)],[(CAND,7),(OUTPUT,3)],[(OUTPUT,4),(OUTPUT,5)],[(OUTPUT,6),(OUTPUT,7)]]
+        written = dict()
+        ig_now, h_now, h_next = [], [], []
+        for step in steps + [[], [], []]:
+            accs = []
+            for k, u in step:
+                acc = psum.tile([PARTS, N_TILE], F32, name="acc", tag="bank")
+                passes(k, u, acc, range(K_GROUPS))
+                accs.append(acc)
+            for u in h_now:
+                nc.vector.tensor_tensor(out=at(OUTPUT, u), in0=at(OUTPUT, u), in1=at(INPUT, u), op=MULT)
+                nc.sync.dma_start(out=h_rows[:, u % M_TILES, cols_of(u)], in_=at(OUTPUT, u))
+            for u in ig_now:
+                nc.vector.tensor_tensor(out=at(CAND, u), in0=at(CAND, u), in1=at(INPUT, u), op=MULT)
+                nc.gpsimd.tensor_tensor(out=at(CAND, u), in0=at(CAND, u), in1=at(FORGET, u), op=ADD)
+            for (k, u), acc in zip(step, accs):
+                empty_bank(k, u, acc)
+                written[(k, u)] = True
+            for u in ig_now:
+                nc.sync.dma_start(out=c_rows[:, u % M_TILES, cols_of(u)], in_=at(CAND, u))
+                nc.scalar.activation(out=at(INPUT, u), in_=at(CAND, u), func=TANH)
+                written[("tanh_c", u)] = True
+            h_now, h_next = h_next, []
+            ig_now = [u for k, u in step if k == CAND]
+            for u in range(UNITS):
+                if (OUTPUT, u) in written and ("tanh_c", u) in written and ("h", u) not in written:
+                    written[("h", u)] = True
+                    h_next.append(u)

@@ -190,7 +190,7 @@ def tile_structuredlstmcell_kernel(
                     nc.gpsimd.tensor_tensor(out=at(FORGET, u), in0=at(FORGET, u), in1=cell_rows[:, u % M_TILES, cols_of(u)], op=MULT)
             spread_bias(next_bias)
 
-        steps = [[(INPUT,4),(INPUT,5)],[(CAND,0),(CAND,1)],[(INPUT,6),(CAND,2)],[(INPUT,7),(CAND,3)],[(CAND,4),(OUTPUT,0)],[(CAND,5),(OUTPUT,1)],[(CAND,6),(OUTPUT,2)],[(CAND,7),(OUTPUT,3)],[(OUTPUT,4),(OUTPUT,5)],[(OUTPUT,6),(OUTPUT,7)]]
+        steps = [[(INPUT,4),(INPUT,5)],[(CAND,0),(CAND,1)],[(INPUT,6),(CAND,2)],[(CAND,3),(OUTPUT,0)],[(INPUT,7),(OUTPUT,1)],[(CAND,4),(OUTPUT,2)],[(CAND,5),(OUTPUT,3)],[(CAND,6),(OUTPUT,4)],[(CAND,7),(OUTPUT,5)],[(OUTPUT,6),(OUTPUT,7)]]
         written = dict()
         ig_now, h_now, h_next = [], [], []
         for step in steps + [[], [], []]:

@@ -190,7 +190,7 @@ def tile_structuredlstmcell_kernel(
                     nc.gpsimd.tensor_tensor(out=at(FORGET, u), in0=at(FORGET, u), in1=cell_rows[:, u % M_TILES, cols_of(u)], op=MULT)
             spread_bias(next_bias)
 
-        steps = [[(INPUT,4),(INPUT,5)],[(CAND,0),(CAND,1)],[(INPUT,6),(CAND,2)],[(CAND,3),(OUTPUT,0)],[(INPUT,7),(OUTPUT,1)],[(CAND,4),(OUTPUT,2)],[(CAND,5),(OUTPUT,3)],[(CAND,6),(OUTPUT,4)],[(CAND,7),(OUTPUT,5)],[(OUTPUT,6),(OUTPUT,7)]]
+        steps = [[(INPUT,4),(INPUT,5)],[(CAND,0),(CAND,1)],[(CAND,2),(CAND,3)],[(CAND,4),(OUTPUT,0)],[(INPUT,6),(OUTPUT,1)],[(CAND,5),(OUTPUT,2)],[(INPUT,7),(OUTPUT,3)],[(CAND,6),(OUTPUT,4)],[(CAND,7),(OUTPUT,5)],[(OUTPUT,6),(OUTPUT,7)]]
         written = dict()
         ig_now, h_now, h_next = [], [], []
         for step in steps + [[], [], []]:

@@ -174,47 +174,43 @@ def tile_structuredlstmcell_kernel(
             nc.vector.tensor_tensor(out=at(k, u), in0=acc[:], in1=bias_all[:, k, cols_of(u)], op=ADD)
             nc.scalar.activation(out=at(k, u), in_=at(k, u), func=gates[k]["func"])
 
-        for k, half, next_bias in ((FORGET, 0, INPUT), (FORGET, 1, CAND), (INPUT, 0, OUTPUT)):
-            units = [half * M_TILES + m for m in range(M_TILES)]
-            accs = [psum.tile([PARTS, N_TILE], F32, name="acc%d" % m, tag="bank") for m in range(M_TILES)]
-            if half == 0:
+        program = "[f0,f1,f2,f3] f0 f1 f2 f3 B1 f4 f5 f6 f7 B2 [i0,i1,i2,i3] i0 i1 i2 i3 B3 i4 i5 g0 g1 G0 c0 g2 g3 T0 G1 c1 G2 c2 g4 o0 T1 G3 c3 G4 c4 i6 o1 T2 g5 o2 T3 i7 T4 H0 H1 G5 c5 o3 g6 o4 T5 H2 H3 G6 c6 g7 o5 T6 o6 H4 G7 o7 C7 T7 H5 H6 H7".split()
+        gate_of = {"f": FORGET, "i": INPUT, "g": CAND, "o": OUTPUT}
+        accs = dict()
+        group = None
+        for tok in program:
+            if tok[0] == "[":
+                names = tok[1:-1].split(",")
+                for x in names:
+                    acc = psum.tile([PARTS, N_TILE], F32, name="acc", tag="bank")
+                    accs[x] = acc
                 for c in range(K_GROUPS):
-                    for m, u in enumerate(units):
-                        passes(k, u, accs[m], [c])
-            else:
-                for m, u in enumerate(units):
-                    passes(k, u, accs[m], range(K_GROUPS))
-            for m, u in enumerate(units):
-                empty_bank(k, u, accs[m])
-                if k == FORGET:
+                    for x in names:
+                        passes(gate_of[x[0]], int(x[1]), accs[x], [c])
+                continue
+            u = int(tok[1])
+            if tok[0] in gate_of:
+                k = gate_of[tok[0]]
+                if tok not in accs:
+                    acc = psum.tile([PARTS, N_TILE], F32, name="acc", tag="bank")
+                    accs[tok] = acc
+                    passes(k, u, acc, range(K_GROUPS))
+                empty_bank(k, u, accs[tok])
+                if k == FORGET and not [].count(u):
                     nc.gpsimd.tensor_tensor(out=at(FORGET, u), in0=at(FORGET, u), in1=cell_rows[:, u % M_TILES, cols_of(u)], op=MULT)
-            spread_bias(next_bias)
-
-        steps = [[(INPUT,4),(INPUT,5)],[(CAND,0),(CAND,1)],[(CAND,2),(CAND,3)],[(CAND,4),(OUTPUT,0)],[(INPUT,6),(OUTPUT,1)],[(CAND,5),(OUTPUT,2)],[(INPUT,7),(OUTPUT,3)],[(CAND,6),(OUTPUT,4)],[(CAND,7),(OUTPUT,5)],[(OUTPUT,6),(OUTPUT,7)]]
-        written = dict()
-        ig_now, h_now, h_next = [], [], []
-        for step in steps + [[], [], []]:
-            accs = []
-            for k, u in step:
-                acc = psum.tile([PARTS, N_TILE], F32, name="acc", tag="bank")
-                passes(k, u, acc, range(K_GROUPS))
-                accs.append(acc)
-            for u in h_now:
-                nc.vector.tensor_tensor(out=at(OUTPUT, u), in0=at(OUTPUT, u), in1=at(INPUT, u), op=MULT)
-                nc.sync.dma_start(out=h_rows[:, u % M_TILES, cols_of(u)], in_=at(OUTPUT, u))
-            for u in ig_now:
+            elif tok[0] == "F":
+                nc.vector.tensor_tensor(out=at(FORGET, u), in0=at(FORGET, u), in1=cell_rows[:, u % M_TILES, cols_of(u)], op=MULT)
+            elif tok[0] == "G":
                 nc.vector.tensor_tensor(out=at(CAND, u), in0=at(CAND, u), in1=at(INPUT, u), op=MULT)
+            elif tok[0] == "c":
                 nc.gpsimd.tensor_tensor(out=at(CAND, u), in0=at(CAND, u), in1=at(FORGET, u), op=ADD)
-            for (k, u), acc in zip(step, accs):
-                empty_bank(k, u, acc)
-                written[(k, u)] = True
-            for u in ig_now:
+            elif tok[0] == "C":
+                nc.vector.tensor_tensor(out=at(CAND, u), in0=at(CAND, u), in1=at(FORGET, u), op=ADD)
+            elif tok[0] == "T":
                 nc.sync.dma_start(out=c_rows[:, u % M_TILES, cols_of(u)], in_=at(CAND, u))
                 nc.scalar.activation(out=at(INPUT, u), in_=at(CAND, u), func=TANH)
-                written[("tanh_c", u)] = True
-            h_now, h_next = h_next, []
-            ig_now = [u for k, u in step if k == CAND]
-            for u in range(UNITS):
-                if (OUTPUT, u) in written and ("tanh_c", u) in written and ("h", u) not in written:
-                    written[("h", u)] = True
-                    h_next.append(u)
+            elif tok[0] == "H":
+                nc.vector.tensor_tensor(out=at(OUTPUT, u), in0=at(OUTPUT, u), in1=at(INPUT, u), op=MULT)
+                nc.sync.dma_start(out=h_rows[:, u % M_TILES, cols_of(u)], in_=at(OUTPUT, u))
+            elif tok[0] == "B":
+                spread_bias(u)

@@ -77,9 +77,10 @@ def tile_structuredlstmcell_kernel(
         bias_all = keep.tile([PARTS, 4, HID], BF16, name="bias_all")
         ones = keep.tile([PARTS, PARTS], BF16, name="ones")
         ident = keep.tile([PARTS, PARTS], F32, name="ident")
-        value = [keep.tile([PARTS, M_TILES, HID], F32, name="value%d" % k) for k in range(4)]
+        value = [keep.tile([PARTS, UNITS, N_TILE], F32, name="value%d" % k) for k in range(4)]
 
-        nc.vector.memset(bias_rows[:], 0.0)
+        for k in range(4):
+            nc.vector.memset(bias_rows[:, k, :], 0.0)
         for s in range(3):
             nc.vector.memset(w_scales[s][:].bitcast(I32), 0)
         nc.vector.memset(ones[:], 1.0)
@@ -109,8 +110,8 @@ def tile_structuredlstmcell_kernel(
             load_x(s)
         for k in range(4):
             for s in range(3):
-                load_codes(k, s)
                 load_scale_rows(k, s)
+                load_codes(k, s)
             if k == FORGET:
                 nc.sync.dma_start(out=cell_rows[:], in_=by_partition(cell))
 
@@ -148,7 +149,9 @@ def tile_structuredlstmcell_kernel(
             if c > 0:
                 quantise(c - 1)
         quantise(K_GROUPS - 1)
-        spread_bias(0)
+
+        for k in [0, 1]:
+            spread_bias(k)
 
         def cols_of(u):
             return slice((u // M_TILES) * N_TILE, (u // M_TILES + 1) * N_TILE)
@@ -174,43 +177,91 @@ def tile_structuredlstmcell_kernel(
             nc.vector.tensor_tensor(out=at(k, u), in0=acc[:], in1=bias_all[:, k, cols_of(u)], op=ADD)
             nc.scalar.activation(out=at(k, u), in_=at(k, u), func=gates[k]["func"])
 
-        program = "[f0,f1,f2,f3] f0 f1 f2 f3 B1 f4 f5 f6 f7 B2 [i0,i1,i2,i3] i0 i1 i2 i3 B3 i4 i5 g0 g1 G0 c0 g2 g3 T0 G1 c1 G2 c2 g4 o0 T1 G3 c3 G4 c4 i6 o1 T2 g5 o2 T3 i7 T4 H0 H1 G5 c5 o3 g6 o4 T5 H2 H3 G6 c6 g7 o5 T6 o6 H4 G7 o7 C7 T7 H5 H6 H7".split()
+        program = "[f0,f1,f2,f3,f4,f5,f6,f7] f0 f1 f2 f3 f4 f5 f6 f7 B2 B3 [i0,i1,i2,i3] i0 i1 i2 i3 i4 i5 g0 g1 G0 c0 g2 g3 T0 G1 c1 G2 c2 g4 o0 T1 G3 c3 G4 c4 i6 o1 T2 g5 o2 T3 i7 T4 H0 H1 G5 c5 o3 g6 o4 T5 H2 H3 G6 c6 g7 o5 T6 o6 H4 G7 o7 C7 T7 H5 H6 H7".split()
         gate_of = {"f": FORGET, "i": INPUT, "g": CAND, "o": OUTPUT}
         accs = dict()
-        group = None
+
+        def cut(word):
+            u = int(word[0])
+            lo = (u // M_TILES) * N_TILE
+            hi = lo + N_TILE
+            if word[-1] == "a":
+                hi -= N_TILE // 2
+            if word[-1] == "b":
+                lo += N_TILE // 2
+            m0 = u % M_TILES
+            m1 = int(word[1]) % M_TILES + 1 if len(word) > 1 and word[1] in "01234567" else m0 + 1
+            return slice(m0, m1), slice(lo, hi)
+
+        def vals(k, word):
+            ms, cols = cut(word)
+            u = int(word[0])
+            lo = cols.start % N_TILE
+            return value[k][:, u:u + ms.stop - ms.start, lo:lo + cols.stop - cols.start]
+
+        def mx(k, word, acc, groups):
+            ms, cols = cut(word)
+            rows = slice(ms.start * PARTS, ms.stop * PARTS)
+            for c in groups:
+                s = source_of[c]
+                nc.tensor.matmul_mx(
+                    out=acc[:],
+                    lhsT=x_codes[:, c, rows].bitcast(FP8X4),
+                    lhsT_scale=x_scales[:, c, rows],
+                    rhs=w_codes[k][s][:, c - sources[s]["first"], cols].bitcast(FP8X4),
+                    rhs_scale=w_scales[s][4 * c:PARTS, k, cols],
+                    start=(c == 0),
+                    stop=(c == K_GROUPS - 1),
+                )
+
+        def open_bank(x):
+            ms, cols = cut(x[1:])
+            acc = psum.tile([PARTS, cols.stop - cols.start], F32, name="acc", tag="bank")
+            accs[x] = acc
+            return acc
+
         for tok in program:
             if tok[0] == "[":
                 names = tok[1:-1].split(",")
                 for x in names:
-                    acc = psum.tile([PARTS, N_TILE], F32, name="acc", tag="bank")
-                    accs[x] = acc
-                for c in range(K_GROUPS):
-                    for x in names:
-                        passes(gate_of[x[0]], int(x[1]), accs[x], [c])
+                    open_bank(x)
+                rounds = [(names[:4], range(K_GROUPS))]
+                if len(names) == 8:
+                    rounds = [(names, [0]), (names[:4], [1, 2, 3])]
+                for who, cs in rounds:
+                    for c in cs:
+                        for x in who:
+                            mx(gate_of[x[0]], x[1:], accs[x], [c])
+                for x in names[4:]:
+                    mx(gate_of[x[0]], x[1:], accs[x], [1, 2, 3])
                 continue
-            u = int(tok[1])
+            w = tok[1:]
             if tok[0] in gate_of:
                 k = gate_of[tok[0]]
                 if tok not in accs:
-                    acc = psum.tile([PARTS, N_TILE], F32, name="acc", tag="bank")
-                    accs[tok] = acc
-                    passes(k, u, acc, range(K_GROUPS))
-                empty_bank(k, u, accs[tok])
-                if k == FORGET and not [].count(u):
-                    nc.gpsimd.tensor_tensor(out=at(FORGET, u), in0=at(FORGET, u), in1=cell_rows[:, u % M_TILES, cols_of(u)], op=MULT)
-            elif tok[0] == "F":
-                nc.vector.tensor_tensor(out=at(FORGET, u), in0=at(FORGET, u), in1=cell_rows[:, u % M_TILES, cols_of(u)], op=MULT)
-            elif tok[0] == "G":
-                nc.vector.tensor_tensor(out=at(CAND, u), in0=at(CAND, u), in1=at(INPUT, u), op=MULT)
-            elif tok[0] == "c":
-                nc.gpsimd.tensor_tensor(out=at(CAND, u), in0=at(CAND, u), in1=at(FORGET, u), op=ADD)
-            elif tok[0] == "C":
-                nc.vector.tensor_tensor(out=at(CAND, u), in0=at(CAND, u), in1=at(FORGET, u), op=ADD)
-            elif tok[0] == "T":
-                nc.sync.dma_start(out=c_rows[:, u % M_TILES, cols_of(u)], in_=at(CAND, u))
-                nc.scalar.activation(out=at(INPUT, u), in_=at(CAND, u), func=TANH)
-            elif tok[0] == "H":
-                nc.vector.tensor_tensor(out=at(OUTPUT, u), in0=at(OUTPUT, u), in1=at(INPUT, u), op=MULT)
-                nc.sync.dma_start(out=h_rows[:, u % M_TILES, cols_of(u)], in_=at(OUTPUT, u))
+                    mx(k, w, open_bank(tok), range(K_GROUPS))
+                ms, cols = cut(w)
+                lo = cols.start % N_TILE
+                v = value[k][:, int(w[0]), lo:lo + cols.stop - cols.start]
+                nc.vector.tensor_tensor(out=v, in0=accs[tok][:], in1=bias_all[:, k, cols], op=ADD)
+                nc.scalar.activation(out=v, in_=v, func=gates[k]["func"])
+                if k == FORGET and tok not in []:
+                    nc.gpsimd.tensor_tensor(out=vals(FORGET, w), in0=vals(FORGET, w), in1=cell_rows[:, ms, cols], op=MULT)
             elif tok[0] == "B":
-                spread_bias(u)
+                spread_bias(int(w))
+            else:
+                ms, cols = cut(w)
+                if tok[0] == "F":
+                    nc.vector.tensor_tensor(out=vals(FORGET, w), in0=vals(FORGET, w), in1=cell_rows[:, ms, cols], op=MULT)
+                elif tok[0] == "G":
+                    nc.vector.tensor_tensor(out=vals(CAND, w), in0=vals(CAND, w), in1=vals(INPUT, w), op=MULT)
+                elif tok[0] == "c":
+                    nc.gpsimd.tensor_tensor(out=vals(CAND, w), in0=vals(CAND, w), in1=vals(FORGET, w), op=ADD)
+                elif tok[0] == "C":
+                    nc.vector.tensor_tensor(out=vals(CAND, w), in0=vals(CAND, w), in1=vals(FORGET, w), op=ADD)
+                elif tok[0] == "T":
+                    nc.sync.dma_start(out=c_rows[:, ms, cols], in_=vals(CAND, w))
+                    nc.scalar.activation(out=vals(INPUT, w), in_=vals(CAND, w), func=TANH)
+                elif tok[0] == "H":
+                    nc.vector.tensor_tensor(out=vals(OUTPUT, w), in0=vals(OUTPUT, w), in1=vals(INPUT, w), op=MULT)
+                    nc.sync.dma_start(out=h_rows[:, ms, cols], in_=vals(OUTPUT, w))

@@ -67,11 +67,11 @@ def tile_structuredlstmcell_kernel(
         psum = ctx.enter_context(tc.psum_pool(name="psum", bufs=8))
 
         x_rows = [keep.tile([PARTS, M_TILES, s["count"] * K_PASS], BF16, name="x_rows%d" % s["first"]) for s in sources]
-        x_codes = keep.tile([PARTS, K_GROUPS, BATCH], U32, name="x_codes", align_bytes=64)
-        x_scales = keep.tile([PARTS, K_GROUPS, BATCH], U8, name="x_scales", align_bytes=64)
-        w_codes = [[keep.tile([PARTS, s["count"], HID], U32, name="w_codes%d_%d" % (k, s["first"]), align_bytes=64)
+        x_codes = keep.tile([PARTS, 0 + K_GROUPS * BATCH], U32, name="x_codes", align_bytes=256)[:, 0:].rearrange("p (c b) -> p c b", c=K_GROUPS)
+        x_scales = keep.tile([PARTS, 64 + K_GROUPS * BATCH], U8, name="x_scales", align_bytes=256)[:, 64:].rearrange("p (c b) -> p c b", c=K_GROUPS)
+        w_codes = [[keep.tile([PARTS, 32 + s["count"] * HID], U32, name="w_codes%d_%d" % (k, s["first"]), align_bytes=256)[:, 32:].rearrange("p (c n) -> p c n", n=HID)
                     for s in sources] for k in range(4)]
-        w_scales = [keep.tile([PARTS, 4, HID], U8, name="w_scales%d" % s["first"], align_bytes=64) for s in sources]
+        w_scales = [keep.tile([PARTS, 192 + 4 * HID], U8, name="w_scales%d" % s["first"], align_bytes=256)[:, 192:].rearrange("p (k n) -> p k n", n=HID) for s in sources]
         cell_rows = keep.tile([PARTS, M_TILES, HID], BF16, name="cell_rows")
         bias_rows = keep.tile([PARTS, 4, HID], BF16, name="bias_rows")
         bias_all = keep.tile([PARTS, 4, HID], BF16, name="bias_all")

@@ -76,14 +76,18 @@ def tile_structuredlstmcell_kernel(
         bias_rows = keep.tile([PARTS, 4, HID], BF16, name="bias_rows")
         bias_all = keep.tile([PARTS, 4, HID], BF16, name="bias_all")
         ones = keep.tile([PARTS, PARTS], BF16, name="ones")
+        idle = keep.tile([PARTS, N_TILE], BF16, name="idle")
         ident = keep.tile([PARTS, PARTS], F32, name="ident")
         value = [keep.tile([PARTS, UNITS, N_TILE], F32, name="value%d" % k) for k in range(4)]
 
-        for k in range(4):
+        nc.vector.memset(bias_rows[:, FORGET, :], 0.0)
+        nc.gpsimd.dma_start(out=bias_rows[0:1, FORGET, :], in_=gates[FORGET]["bias"].unsqueeze(0))
+        nc.vector.memset(ones[:], 1.0)
+        nc.vector.memset(idle[:], 0.0)
+        for k in (INPUT, CAND, OUTPUT):
             nc.vector.memset(bias_rows[:, k, :], 0.0)
         for s in range(3):
             nc.vector.memset(w_scales[s][:].bitcast(I32), 0)
-        nc.vector.memset(ones[:], 1.0)
         make_identity(nc, ident[:])
 
         def load_x(s):
@@ -103,7 +107,7 @@ def tile_structuredlstmcell_kernel(
                 in_=gates[k]["words"][s].rearrange("g p n t -> p g (n t)").bitcast(I32),
             )
 
-        for k in range(4):
+        for k in (INPUT, CAND, OUTPUT):
             nc.gpsimd.dma_start(out=bias_rows[0:1, k, :], in_=gates[k]["bias"].unsqueeze(0))
 
         for s in range(3):
@@ -127,6 +131,12 @@ def tile_structuredlstmcell_kernel(
         def quantise(c):
             nc.vector.quantize_mx(out=x_codes[:, c, :].bitcast(FP8X4), scales=x_scales[:, c, :], in_=grouped[c][:])
 
+        def keep_busy(times):
+            waste = psum.tile([PARTS, N_TILE], F32, name="waste", tag="bank")
+            for n in range(times):
+                nc.tensor.matmul(out=waste[:], lhsT=ones[:], rhs=idle[:], start=True, stop=True)
+
+        keep_busy(5)
         for c in range(K_GROUPS):
             s = source_of[c]
             word0 = (c - sources[s]["first"]) * K_PASS // 2
@@ -146,12 +156,14 @@ def tile_structuredlstmcell_kernel(
                     nc.vector.tensor_copy(out=grouped_words[:, rows, :], in_=flipped[:].rearrange("p u b -> p b u"))
                 else:
                     nc.scalar.copy(out=grouped_words[:, rows, :], in_=flipped[:].rearrange("p u b -> p b u"))
+            if c < 2:
+                keep_busy(2)
+            else:
+                spread_bias(c - 2)
             if c > 0:
                 quantise(c - 1)
         quantise(K_GROUPS - 1)
 
-        for k in [0, 1]:
-            spread_bias(k)
 
         def cols_of(u):
             return slice((u // M_TILES) * N_TILE, (u // M_TILES + 1) * N_TILE)
@@ -177,7 +189,7 @@ def tile_structuredlstmcell_kernel(
             nc.vector.tensor_tensor(out=at(k, u), in0=acc[:], in1=bias_all[:, k, cols_of(u)], op=ADD)
             nc.scalar.activation(out=at(k, u), in_=at(k, u), func=gates[k]["func"])
 
-        program = "[f0,f1,f2,f3,f4,f5,f6,f7] f0 f1 f2 f3 f4 f5 f6 f7 B2 B3 [i0,i1,i2,i3] i0 i1 i2 i3 i4 i5 g0 g1 G0 c0 g2 g3 T0 G1 c1 G2 c2 g4 o0 T1 G3 c3 G4 c4 i6 o1 T2 g5 o2 T3 i7 T4 H0 H1 G5 c5 o3 g6 o4 T5 H2 H3 G6 c6 g7 o5 T6 o6 H4 G7 o7 C7 T7 H5 H6 H7".split()
+        program = "[f0,f1,f2,f3,f4,f5,f6,f7] f0 f1 f2 f3 f4 f5 f6 f7 B2 B3 [i0,i1,i2,i3] i0 i1 i2 i3 i4 i5 g0 g1 G0 c0 g2 g3 T0 G1 c1 G2 c2 g4 o0 T1 G3 C3 T3 G4 c4 i6 o1 T2 g5 o2 i7 T4 H0 H1 G5 c5 o3 g6 o4 T5 H2 H3 G6 c6 g7 o5 T6 o6 H4 G7 o7 C7 T7 H5 H6 H7".split()
         gate_of = {"f": FORGET, "i": INPUT, "g": CAND, "o": OUTPUT}
         accs = dict()
 

@@ -81,9 +81,11 @@ def tile_structuredlstmcell_kernel(
         value = [keep.tile([PARTS, UNITS, N_TILE], F32, name="value%d" % k) for k in range(4)]
 
         nc.vector.memset(bias_rows[:, FORGET, :], 0.0)
-        nc.gpsimd.dma_start(out=bias_rows[0:1, FORGET, :], in_=gates[FORGET]["bias"].unsqueeze(0))
+        nc.scalar.dma_start(out=bias_rows[0:1, FORGET, :], in_=gates[FORGET]["bias"].unsqueeze(0))
         nc.vector.memset(ones[:], 1.0)
         nc.vector.memset(idle[:], 0.0)
+        early = keep.tile([PARTS, 1], F32, name="early")
+        nc.scalar.activation(out=early[:], in_=ones[:, 0:1], func=SIGMOID)
         for k in (INPUT, CAND, OUTPUT):
             nc.vector.memset(bias_rows[:, k, :], 0.0)
         for s in range(3):
@@ -91,7 +93,9 @@ def tile_structuredlstmcell_kernel(
         make_identity(nc, ident[:])
 
         def load_x(s):
-            nc.sync.dma_start(out=x_rows[s][:], in_=by_partition(sources[s]["x"]))
+            for part in range(sources[s]["count"]):
+                m = slice(part * M_TILES // sources[s]["count"], (part + 1) * M_TILES // sources[s]["count"])
+                nc.sync.dma_start(out=x_rows[s][:, m, :], in_=by_partition(sources[s]["x"])[:, m, :])
 
         def load_scale_rows(k, s):
             first, count = sources[s]["first"], sources[s]["count"]
@@ -137,33 +141,34 @@ def tile_structuredlstmcell_kernel(
                 nc.tensor.matmul(out=waste[:], lhsT=ones[:], rhs=idle[:], start=True, stop=True)
 
         keep_busy(5)
-        for c in range(K_GROUPS):
+        def flip(c, pair):
             s = source_of[c]
             word0 = (c - sources[s]["first"]) * K_PASS // 2
             x_words = x_rows[s][:].bitcast(F32)
             grouped_words = grouped[c][:].bitcast(F32).rearrange("p (b u) -> p b u", u=2)
-            for pair in range(M_TILES // 2):
-                flipped = psum.tile([PARTS, 2, 2 * PARTS], F32, name="flipped", tag="bank")
-                for u in range(2):
-                    for j in range(2):
-                        nc.tensor.transpose(
-                            flipped[:, u, j * PARTS:(j + 1) * PARTS],
-                            x_words[:, 2 * pair + j, word0 + u:word0 + K_PASS // 2:2],
-                            ident[:],
-                        )
-                rows = slice(pair * 2 * PARTS, (pair + 1) * 2 * PARTS)
-                if pair == 0:
-                    nc.vector.tensor_copy(out=grouped_words[:, rows, :], in_=flipped[:].rearrange("p u b -> p b u"))
-                else:
-                    nc.scalar.copy(out=grouped_words[:, rows, :], in_=flipped[:].rearrange("p u b -> p b u"))
-            if c < 2:
-                keep_busy(2)
+            flipped = psum.tile([PARTS, 2, 2 * PARTS], F32, name="flipped", tag="bank")
+            for u in range(2):
+                for j in range(2):
+                    nc.tensor.transpose(
+                        flipped[:, u, j * PARTS:(j + 1) * PARTS],
+                        x_words[:, 2 * pair + j, word0 + u:word0 + K_PASS // 2:2],
+                        ident[:],
+                    )
+            rows = slice(pair * 2 * PARTS, (pair + 1) * 2 * PARTS)
+            if (c + pair) % 2 == 0 if c in (1, 2) else pair == 0:
+                nc.vector.tensor_copy(out=grouped_words[:, rows, :], in_=flipped[:].rearrange("p u b -> p b u"))
             else:
-                spread_bias(c - 2)
-            if c > 0:
-                quantise(c - 1)
-        quantise(K_GROUPS - 1)
+                nc.scalar.copy(out=grouped_words[:, rows, :], in_=flipped[:].rearrange("p u b -> p b u"))
 
+        for step in "t00 t01 t10 t20 q0 d2 t11 t21 B0 q1 t30 t31 q2 B1 q3".split():
+            if step[0] == "t":
+                flip(int(step[1]), int(step[2]))
+            elif step[0] == "q":
+                quantise(int(step[1]))
+            elif step[0] == "d":
+                keep_busy(int(step[1]))
+            else:
+                spread_bias(int(step[1]))
 
         def cols_of(u):
             return slice((u // M_TILES) * N_TILE, (u // M_TILES + 1) * N_TILE)

@@ -97,12 +97,12 @@ def tile_structuredlstmcell_kernel(
                 m = slice(part * M_TILES // sources[s]["count"], (part + 1) * M_TILES // sources[s]["count"])
                 nc.sync.dma_start(out=x_rows[s][:, m, :], in_=by_partition(sources[s]["x"])[:, m, :])
 
-        def load_scale_rows(k, s):
+        def load_scale_rows(k, s, queue=nc.sync, view=I32):
             first, count = sources[s]["first"], sources[s]["count"]
             for quad in range(QUADS):
-                nc.sync.dma_start(
-                    out=w_scales[s][32 * quad + 4 * first:32 * quad + 4 * (first + count), k, :].bitcast(I32),
-                    in_=gates[k]["scales"][s][:, 4 * quad:4 * quad + 4, :].bitcast(I32),
+                queue.dma_start(
+                    out=w_scales[s][32 * quad + 4 * first:32 * quad + 4 * (first + count), k, :].bitcast(view),
+                    in_=gates[k]["scales"][s][:, 4 * quad:4 * quad + 4, :].bitcast(view),
                 )
 
         def load_codes(k, s):
@@ -114,11 +114,16 @@ def tile_structuredlstmcell_kernel(
         for k in (INPUT, CAND, OUTPUT):
             nc.gpsimd.dma_start(out=bias_rows[0:1, k, :], in_=gates[k]["bias"].unsqueeze(0))
 
+        on_gpsimd = [(2, 0)]
+        for k, s in on_gpsimd:
+            load_scale_rows(k, s, queue=nc.gpsimd, view=F32)
+
         for s in range(3):
             load_x(s)
         for k in range(4):
             for s in range(3):
-                load_scale_rows(k, s)
+                if (k, s) not in on_gpsimd:
+                    load_scale_rows(k, s)
                 load_codes(k, s)
             if k == FORGET:
                 nc.sync.dma_start(out=cell_rows[:], in_=by_partition(cell))
@@ -194,7 +199,7 @@ def tile_structuredlstmcell_kernel(
             nc.vector.tensor_tensor(out=at(k, u), in0=acc[:], in1=bias_all[:, k, cols_of(u)], op=ADD)
             nc.scalar.activation(out=at(k, u), in_=at(k, u), func=gates[k]["func"])
 
-        program = "[f0,f1,f2,f3,f4,f5,f6,f7] f0 f1 f2 f3 f4 f5 f6 f7 B2 B3 [i0,i1,i2,i3] i0 i1 i2 i3 i4 i5 g0 g1 G0 c0 g2 g3 T0 G1 c1 G2 c2 g4 o0 T1 G3 C3 T3 G4 c4 i6 o1 T2 g5 o2 i7 T4 H0 H1 G5 c5 o3 g6 o4 T5 H2 H3 G6 c6 g7 o5 T6 o6 H4 G7 o7 C7 T7 H5 H6 H7".split()
+        program = "[f0,f1,f2,f3,f4,f5] f0 f1 f2 f3 f4 f5 f6 f7 [i0,i1,i2,i3] i0 i1 i2 i3 i4 i5 g0 g1 G0 c0 g2 g3 T0 G1 c1 G2 c2 g4 o0 T1 G3 C3 T3 G4 c4 i6 o1 T2 g5 o2 i7 T4 H0 H1 G5 c5 o3 g6 o4 T5 H2 H3 G6 c6 g7 o5 T6 o6 H4 G7 o7 C7 T7 H5 H6 H7".split()
         gate_of = {"f": FORGET, "i": INPUT, "g": CAND, "o": OUTPUT}
         accs = dict()
 
@@ -243,12 +248,15 @@ def tile_structuredlstmcell_kernel(
                 for x in names:
                     open_bank(x)
                 rounds = [(names[:4], range(K_GROUPS))]
-                if len(names) == 8:
+                if len(names) == 6:
                     rounds = [(names, [0]), (names[:4], [1, 2, 3])]
                 for who, cs in rounds:
                     for c in cs:
                         for x in who:
                             mx(gate_of[x[0]], x[1:], accs[x], [c])
+                    if who is names:
+                        spread_bias(CAND)
+                        spread_bias(OUTPUT)
                 for x in names[4:]:
                     mx(gate_of[x[0]], x[1:], accs[x], [1, 2, 3])
                 continue

from contextlib import ExitStack

import concourse.mybir as mybir
from concourse.masks import make_identity

F32 = mybir.dt.float32
BF16 = mybir.dt.bfloat16
I32 = mybir.dt.int32
U32 = mybir.dt.uint32
U8 = mybir.dt.uint8
FP8X4 = mybir.dt.float8_e4m3fn_x4
ADD = mybir.AluOpType.add
MULT = mybir.AluOpType.mult
SIGMOID = mybir.ActivationFunctionType.Sigmoid
TANH = mybir.ActivationFunctionType.Tanh

PARTS = 128
BATCH = 512
HID = 1024
K_PASS = 512
K_GROUPS = 4
M_TILES = BATCH // PARTS
N_TILE = 512
HALVES = HID // N_TILE
QUADS = 4
UNITS = HALVES * M_TILES

FLOPS = 2 * BATCH * (K_GROUPS * K_PASS) * (4 * HID)


def tile_structuredlstmcell_kernel(
    tc, P, hidden, cell, ext_input,
    W_pi_words, W_pi_scales, b_pi, W_pf_words, W_pf_scales, b_pf,
    W_pg_words, W_pg_scales, b_pg, W_po_words, W_po_scales, b_po,
    W_hi_words, W_hi_scales, W_hf_words, W_hf_scales,
    W_hg_words, W_hg_scales, W_ho_words, W_ho_scales,
    W_xi_words, W_xi_scales, W_xf_words, W_xf_scales,
    W_xg_words, W_xg_scales, W_xo_words, W_xo_scales,
    out_0, out_1,
):
    nc = tc.nc

    gates = [
        dict(func=SIGMOID, bias=b_pf, words=(W_pf_words, W_hf_words, W_xf_words),
             scales=(W_pf_scales, W_hf_scales, W_xf_scales)),
        dict(func=SIGMOID, bias=b_pi, words=(W_pi_words, W_hi_words, W_xi_words),
             scales=(W_pi_scales, W_hi_scales, W_xi_scales)),
        dict(func=TANH, bias=b_pg, words=(W_pg_words, W_hg_words, W_xg_words),
             scales=(W_pg_scales, W_hg_scales, W_xg_scales)),
        dict(func=SIGMOID, bias=b_po, words=(W_po_words, W_ho_words, W_xo_words),
             scales=(W_po_scales, W_ho_scales, W_xo_scales)),
    ]
    FORGET, INPUT, CAND, OUTPUT = 0, 1, 2, 3
    sources = [dict(x=P, first=0, count=1), dict(x=hidden, first=1, count=2), dict(x=ext_input, first=3, count=1)]
    source_of = [0, 1, 1, 2]

    def by_partition(ap):
        return ap.rearrange("(p m) n -> p m n", m=M_TILES)

    h_rows = by_partition(out_0)
    c_rows = by_partition(out_1)

    with ExitStack() as ctx:
        ctx.enter_context(tc.manual_schedule())
        keep = ctx.enter_context(tc.tile_pool(name="keep", bufs=1))
        stage = ctx.enter_context(tc.tile_pool(name="stage", bufs=K_GROUPS))
        psum = ctx.enter_context(tc.psum_pool(name="psum", bufs=8))

        x_rows = [keep.tile([PARTS, M_TILES, s["count"] * K_PASS], BF16, name="x_rows%d" % s["first"]) for s in sources]
        x_codes = keep.tile([PARTS, 0 + K_GROUPS * BATCH], U32, name="x_codes", align_bytes=256)[:, 0:].rearrange("p (c b) -> p c b", c=K_GROUPS)
        x_scales = keep.tile([PARTS, 64 + K_GROUPS * BATCH], U8, name="x_scales", align_bytes=256)[:, 64:].rearrange("p (c b) -> p c b", c=K_GROUPS)
        w_codes = [[keep.tile([PARTS, 32 + s["count"] * HID], U32, name="w_codes%d_%d" % (k, s["first"]), align_bytes=256)[:, 32:].rearrange("p (c n) -> p c n", n=HID)
                    for s in sources] for k in range(4)]
        w_scales = [keep.tile([PARTS, 192 + 4 * HID], U8, name="w_scales%d" % s["first"], align_bytes=256)[:, 192:].rearrange("p (k n) -> p k n", n=HID) for s in sources]
        cell_rows = keep.tile([PARTS, M_TILES, HID], BF16, name="cell_rows")
        bias_rows = keep.tile([PARTS, 4, HID], BF16, name="bias_rows")
        bias_all = keep.tile([PARTS, 4, HID], BF16, name="bias_all")
        ones = keep.tile([PARTS, PARTS], BF16, name="ones")
        idle = keep.tile([PARTS, N_TILE], BF16, name="idle")
        ident = keep.tile([PARTS, PARTS], F32, name="ident")
        value = [keep.tile([PARTS, UNITS, N_TILE], F32, name="value%d" % k) for k in range(4)]

        nc.vector.memset(bias_rows[:, FORGET, :], 0.0)
        nc.scalar.dma_start(out=bias_rows[0:1, FORGET, :], in_=gates[FORGET]["bias"].unsqueeze(0))
        nc.vector.memset(ones[:], 1.0)
        nc.vector.memset(idle[:], 0.0)
        early = keep.tile([PARTS, 1], F32, name="early")
        nc.scalar.activation(out=early[:], in_=ones[:, 0:1], func=SIGMOID)
        for k in (INPUT, CAND, OUTPUT):
            nc.vector.memset(bias_rows[:, k, :], 0.0)
        for s in range(3):
            nc.vector.memset(w_scales[s][:].bitcast(I32), 0)
        make_identity(nc, ident[:])

        def load_x(s):
            for part in range(sources[s]["count"]):
                m = slice(part * M_TILES // sources[s]["count"], (part + 1) * M_TILES // sources[s]["count"])
                nc.sync.dma_start(out=x_rows[s][:, m, :], in_=by_partition(sources[s]["x"])[:, m, :])

        def load_scale_rows(k, s, queue=nc.sync, view=I32):
            first, count = sources[s]["first"], sources[s]["count"]
            for quad in range(QUADS):
                queue.dma_start(
                    out=w_scales[s][32 * quad + 4 * first:32 * quad + 4 * (first + count), k, :].bitcast(view),
                    in_=gates[k]["scales"][s][:, 4 * quad:4 * quad + 4, :].bitcast(view),
                )

        def load_codes(k, s):
            nc.sync.dma_start(
                out=w_codes[k][s][:].bitcast(I32),
                in_=gates[k]["words"][s].rearrange("g p n t -> p g (n t)").bitcast(I32),
            )

        for k in (INPUT, CAND, OUTPUT):
            nc.gpsimd.dma_start(out=bias_rows[0:1, k, :], in_=gates[k]["bias"].unsqueeze(0))

        on_gpsimd = [(2, 0)]
        for k, s in on_gpsimd:
            load_scale_rows(k, s, queue=nc.gpsimd, view=F32)

        for s in range(3):
            load_x(s)
        for k in range(4):
            for s in range(3):
                if (k, s) not in on_gpsimd:
                    load_scale_rows(k, s)
                load_codes(k, s)
            if k == FORGET:
                nc.sync.dma_start(out=cell_rows[:], in_=by_partition(cell))

        def spread_bias(k):
            spread = psum.tile([PARTS, HID], BF16, name="spread", tag="bank")
            for half in range(HALVES):
                cols = slice(half * N_TILE, (half + 1) * N_TILE)
                nc.tensor.matmul(out=spread[:, cols], lhsT=ones[:], rhs=bias_rows[:, k, cols], start=True, stop=True)
            nc.scalar.copy(out=bias_all[:, k, :], in_=spread[:])

        grouped = [stage.tile([PARTS, 4 * BATCH], BF16, name="grouped", align_bytes=64) for c in range(K_GROUPS)]

        def quantise(c):
            nc.vector.quantize_mx(out=x_codes[:, c, :].bitcast(FP8X4), scales=x_scales[:, c, :], in_=grouped[c][:])

        def keep_busy(times):
            waste = psum.tile([PARTS, N_TILE], F32, name="waste", tag="bank")
            for n in range(times):
                nc.tensor.matmul(out=waste[:], lhsT=ones[:], rhs=idle[:], start=True, stop=True)

        keep_busy(5)
        def flip(c, pair):
            s = source_of[c]
            word0 = (c - sources[s]["first"]) * K_PASS // 2
            x_words = x_rows[s][:].bitcast(F32)
            grouped_words = grouped[c][:].bitcast(F32).rearrange("p (b u) -> p b u", u=2)
            flipped = psum.tile([PARTS, 2, 2 * PARTS], F32, name="flipped", tag="bank")
            for u in range(2):
                for j in range(2):
                    nc.tensor.transpose(
                        flipped[:, u, j * PARTS:(j + 1) * PARTS],
                        x_words[:, 2 * pair + j, word0 + u:word0 + K_PASS // 2:2],
                        ident[:],
                    )
            rows = slice(pair * 2 * PARTS, (pair + 1) * 2 * PARTS)
            if (c + pair) % 2 == 0 if c in (1, 2) else pair == 0:
                nc.vector.tensor_copy(out=grouped_words[:, rows, :], in_=flipped[:].rearrange("p u b -> p b u"))
            else:
                nc.scalar.copy(out=grouped_words[:, rows, :], in_=flipped[:].rearrange("p u b -> p b u"))

        for step in "t00 t01 t10 t20 q0 d2 t11 t21 B0 q1 t30 t31 q2 B1 q3".split():
            if step[0] == "t":
                flip(int(step[1]), int(step[2]))
            elif step[0] == "q":
                quantise(int(step[1]))
            elif step[0] == "d":
                keep_busy(int(step[1]))
            else:
                spread_bias(int(step[1]))

        def cols_of(u):
            return slice((u // M_TILES) * N_TILE, (u // M_TILES + 1) * N_TILE)

        def at(k, u):
            return value[k][:, u % M_TILES, cols_of(u)]

        def passes(k, u, acc, groups):
            rows = slice((u % M_TILES) * PARTS, (u % M_TILES + 1) * PARTS)
            for c in groups:
                s = source_of[c]
                nc.tensor.matmul_mx(
                    out=acc[:],
                    lhsT=x_codes[:, c, rows].bitcast(FP8X4),
                    lhsT_scale=x_scales[:, c, rows],
                    rhs=w_codes[k][s][:, c - sources[s]["first"], cols_of(u)].bitcast(FP8X4),
                    rhs_scale=w_scales[s][4 * c:PARTS, k, cols_of(u)],
                    start=(c == 0),
                    stop=(c == K_GROUPS - 1),
                )

        def empty_bank(k, u, acc):
            nc.vector.tensor_tensor(out=at(k, u), in0=acc[:], in1=bias_all[:, k, cols_of(u)], op=ADD)
            nc.scalar.activation(out=at(k, u), in_=at(k, u), func=gates[k]["func"])

        program = "[f0,f1,f2,f3,f4,f5] f0 f1 f2 f3 f4 f5 f6 f7 [i0,i1,i2,i3] i0 i1 i2 i3 i4 i5 g0 g1 G0 c0 g2 g3 T0 G1 c1 G2 c2 g4 o0 T1 G3 C3 T3 G4 c4 i6 o1 T2 g5 o2 i7 T4 H0 H1 G5 c5 o3 g6 o4 T5 H2 H3 G6 c6 g7 o5 T6 o6 H4 G7 o7 C7 T7 H5 H6 H7".split()
        gate_of = {"f": FORGET, "i": INPUT, "g": CAND, "o": OUTPUT}
        accs = dict()

        def cut(word):
            u = int(word[0])
            lo = (u // M_TILES) * N_TILE
            hi = lo + N_TILE
            if word[-1] == "a":
                hi -= N_TILE // 2
            if word[-1] == "b":
                lo += N_TILE // 2
            m0 = u % M_TILES
            m1 = int(word[1]) % M_TILES + 1 if len(word) > 1 and word[1] in "01234567" else m0 + 1
            return slice(m0, m1), slice(lo, hi)

        def vals(k, word):
            ms, cols = cut(word)
            u = int(word[0])
            lo = cols.start % N_TILE
            return value[k][:, u:u + ms.stop - ms.start, lo:lo + cols.stop - cols.start]

        def mx(k, word, acc, groups):
            ms, cols = cut(word)
            rows = slice(ms.start * PARTS, ms.stop * PARTS)
            for c in groups:
                s = source_of[c]
                nc.tensor.matmul_mx(
                    out=acc[:],
                    lhsT=x_codes[:, c, rows].bitcast(FP8X4),
                    lhsT_scale=x_scales[:, c, rows],
                    rhs=w_codes[k][s][:, c - sources[s]["first"], cols].bitcast(FP8X4),
                    rhs_scale=w_scales[s][4 * c:PARTS, k, cols],
                    start=(c == 0),
                    stop=(c == K_GROUPS - 1),
                )

        def open_bank(x):
            ms, cols = cut(x[1:])
            acc = psum.tile([PARTS, cols.stop - cols.start], F32, name="acc", tag="bank")
            accs[x] = acc
            return acc

        for tok in program:
            if tok[0] == "[":
                names = tok[1:-1].split(",")
                for x in names:
                    open_bank(x)
                rounds = [(names[:4], range(K_GROUPS))]
                if len(names) == 6:
                    rounds = [(names, [0]), (names[:4], [1, 2, 3])]
                for who, cs in rounds:
                    for c in cs:
                        for x in who:
                            mx(gate_of[x[0]], x[1:], accs[x], [c])
                    if who is names:
                        spread_bias(CAND)
                        spread_bias(OUTPUT)
                for x in names[4:]:
                    mx(gate_of[x[0]], x[1:], accs[x], [1, 2, 3])
                continue
            w = tok[1:]
            if tok[0] in gate_of:
                k = gate_of[tok[0]]
                if tok not in accs:
                    mx(k, w, open_bank(tok), range(K_GROUPS))
                ms, cols = cut(w)
                lo = cols.start % N_TILE
                v = value[k][:, int(w[0]), lo:lo + cols.stop - cols.start]
                nc.vector.tensor_tensor(out=v, in0=accs[tok][:], in1=bias_all[:, k, cols], op=ADD)
                nc.scalar.activation(out=v, in_=v, func=gates[k]["func"])
                if k == FORGET and tok not in []:
                    nc.gpsimd.tensor_tensor(out=vals(FORGET, w), in0=vals(FORGET, w), in1=cell_rows[:, ms, cols], op=MULT)
            elif tok[0] == "B":
                spread_bias(int(w))
            else:
                ms, cols = cut(w)
                if tok[0] == "F":
                    nc.vector.tensor_tensor(out=vals(FORGET, w), in0=vals(FORGET, w), in1=cell_rows[:, ms, cols], op=MULT)
                elif tok[0] == "G":
                    nc.vector.tensor_tensor(out=vals(CAND, w), in0=vals(CAND, w), in1=vals(INPUT, w), op=MULT)
                elif tok[0] == "c":
                    nc.gpsimd.tensor_tensor(out=vals(CAND, w), in0=vals(CAND, w), in1=vals(FORGET, w), op=ADD)
                elif tok[0] == "C":
                    nc.vector.tensor_tensor(out=vals(CAND, w), in0=vals(CAND, w), in1=vals(FORGET, w), op=ADD)
                elif tok[0] == "T":
                    nc.sync.dma_start(out=c_rows[:, ms, cols], in_=vals(CAND, w))
                    nc.scalar.activation(out=vals(INPUT, w), in_=vals(CAND, w), func=TANH)
                elif tok[0] == "H":
                    nc.vector.tensor_tensor(out=vals(OUTPUT, w), in0=vals(OUTPUT, w), in1=vals(INPUT, w), op=MULT)
                    nc.sync.dma_start(out=h_rows[:, ms, cols], in_=vals(OUTPUT, w))
